import numpy as np
import ml_dtypes


def mxq(x, axis, fmt="e4m3"):
    dtype, down = {"e4m3": (ml_dtypes.float8_e4m3fn, 7), "e5m2": (ml_dtypes.float8_e5m2, 14)}[fmt]
    v = np.moveaxis(np.asarray(x, np.float32).astype(ml_dtypes.bfloat16).astype(np.float64), axis, -1)
    blocks = v.reshape(v.shape[:-1] + (-1, 32))
    amax = np.abs(blocks).max(-1, keepdims=True)
    byte = np.maximum(np.where(amax > 0, np.frexp(amax)[1] - 1 + 127, 0) - down, 1)
    scale = np.exp2(byte - 127.0)
    codes = (blocks / scale).astype(np.float32).astype(dtype).astype(np.float64)
    return np.moveaxis((codes * scale).reshape(v.shape), -1, axis)


WIDE = False


def mx_kscale(k):
    if not WIDE:
        return np.ones(k)
    levels = np.array([10, -10, 5, -5, 0])
    if k % 512:
        return np.exp2(np.random.permutation(np.resize(levels, k // 32))).repeat(32)
    a = np.empty((k // 512, 16))
    for p in range(k // 512):
        a[p, :8] = np.random.permutation(np.resize(levels, 8))
        for g in range(8):
            far = levels[np.abs(levels - a[p, g]) >= 10]
            a[p, g + 8] = far[np.random.randint(len(far))]
    return np.exp2(a.ravel()).repeat(32)


BF16 = ml_dtypes.bfloat16


def bf(x):
    return np.asarray(x, np.float32).astype(BF16)


def f64(x):
    return np.asarray(x).astype(np.float64)


B, S, N, D = 2, 2, 1024, 512


def draw0():
    s, t = mx_kscale(D), mx_kscale(D)
    return {"tensor0": bf(np.random.standard_normal((S, N, D)) * s),
            "tensor1": bf(np.random.standard_normal((S, N, D)) * 0.5 / t),
            "kernel": bf(np.random.standard_normal((D, D)) * D ** -0.75 * t[:, None] / s[None, :]),
            "bias": bf(0.5 + 0.1 * np.random.standard_normal(1))}


def core(tensor0, tensor1, kernel, bias):
    q = mxq(f64(tensor0), 2, "e4m3") @ mxq(f64(kernel), 1, "e4m3").T
    out = mxq(f64(tensor1), 2, "e4m3") @ mxq(q, 2, "e4m3").transpose(0, 2, 1)
    out = out + f64(bias)
    return np.ascontiguousarray(np.broadcast_to(out[None], (B,) + out.shape))


def e4m3fn_bytes(y):
    return np.clip(np.asarray(y, np.float64), -448.0, 448.0).astype(np.float32).astype(ml_dtypes.float8_e4m3fn).view(np.uint8)


def e4m3fn_values(b):
    return np.asarray(b, np.uint8).view(ml_dtypes.float8_e4m3fn).astype(np.float64)


def setup_inputs():
    d = draw0()
    x0 = np.asarray(d['tensor1']).astype(np.float64)
    s = (np.max(np.abs(x0), axis=(0, 1), keepdims=True) / 448.0).astype(np.float32)
    out = {}
    for k, v in d.items():
        if k == 'tensor1':
            out['tensor1_bytes'] = e4m3fn_bytes(x0 / s.astype(np.float64))
            out['tensor1_scale'] = s
        else:
            out[k] = v
    return out


def reference(tensor0, tensor1_bytes, tensor1_scale, kernel, bias):
    return core(tensor0, e4m3fn_values(tensor1_bytes) * tensor1_scale.astype(np.float64), kernel, bias)

@@ -1,0 +1,410 @@
+from contextlib import ExitStack
+
+import concourse.mybir as mybir
+from concourse.masks import make_identity
+
+F32 = mybir.dt.float32
+BF16 = mybir.dt.bfloat16
+U32 = mybir.dt.uint32
+U8 = mybir.dt.uint8
+FP8 = mybir.dt.float8_e4m3fn
+FP8X4 = mybir.dt.float8_e4m3fn_x4
+ACT = mybir.ActivationFunctionType
+ALU = mybir.AluOpType
+
+P = 128
+S, N, D = 2, 1024, 512
+FLOPS = 2 * S * N * D * D + 2 * S * N * N * D
+
+
+def tile_bilinear_kernel(tc, tensor0, tensor1_bytes, tensor1_scale, kernel, bias, out):
+    nc = tc.nc
+    with ExitStack() as ctx:
+        keep = ctx.enter_context(tc.tile_pool(name="keep", bufs=1))
+        psum = ctx.enter_context(tc.psum_pool(name="psum", bufs=8))
+
+        def sb(name, shape, dtype):
+            return keep.tile(shape, dtype, name=name, align_bytes=64)
+
+        def bank():
+            return psum.tile([P, 512], F32, name="bank")
+
+        ident = sb("ident", [P, P], F32)
+        scale_sb = sb("scale_sb", [P, 4], F32)
+        bias_bf = sb("bias_bf", [P, 1], BF16)
+        bias_sb = sb("bias_sb", [P, 1], F32)
+        warm = sb("warm", [P, 1], F32)
+        warm_out = sb("warm_out", [P, 1], F32)
+        k_sb = sb("k_sb", [P, 4, D], BF16)
+        a_sb = [sb("a_sb%d" % s, [P, 4, 2, D], BF16) for s in range(S)]
+        b_sb = [sb("b_sb%d" % s, [P, 8, D], U8) for s in range(S)]
+        k_codes = sb("k_codes", [P, D], U32)
+        k_scales = sb("k_scales", [P, D], U8)
+        q_codes = [sb("q_codes%d" % s, [P, N], U32) for s in range(S)]
+        q_scales = [sb("q_scales%d" % s, [P, N], U8) for s in range(S)]
+        a_codes, a_scales, b_codes, b_scales = {}, {}, {}, {}
+        banks, grouped, wide, outs = {}, {}, {}, {}
+
+        a_in = tensor0.rearrange("s (g p r) e -> s p g r e", p=P, r=2)
+        b_in = tensor1_bytes.rearrange("s (p r) d -> s p r d", r=8)
+        pair_view = out.rearrange("b s (p h r) j -> s h p b (r j)", h=4, r=2)
+        out_view = out.rearrange("b s (p r) j -> s r p b j", r=8)
+
+        with tc.manual_schedule():
+            nc.scalar.dma_start(out=scale_sb[:], in_=tensor1_scale.rearrange("a b (p t) -> p (a b t)", t=4))
+            nc.scalar.dma_start(out=bias_bf[:], in_=bias.partition_broadcast(P))
+            k_in = kernel.rearrange("(p t) e -> p t e", t=4)
+            nc.sync.dma_start(out=k_sb[:, 0:2, :], in_=k_in[:, 0:2, :])
+            nc.sync.dma_start(out=k_sb[:, 2:4, :], in_=k_in[:, 2:4, :])
+            nc.sync.dma_start(out=a_sb[0][:, 0], in_=a_in[0][:, 0])
+            nc.sync.dma_start(out=b_sb[0][:, 0:2, :], in_=b_in[0][:, 0:2, :])
+            nc.sync.dma_start(out=a_sb[0][:, 1], in_=a_in[0][:, 1])
+            nc.sync.dma_start(out=b_sb[0][:, 2:8, :], in_=b_in[0][:, 2:8, :])
+            nc.sync.dma_start(out=a_sb[0][:, 2:4], in_=a_in[0][:, 2:4])
+            nc.sync.dma_start(out=a_sb[1][:], in_=a_in[1])
+            nc.sync.dma_start(out=b_sb[1][:], in_=b_in[1])
+            make_identity(nc, ident[:])
+            nc.gpsimd.memset(warm[:], 0.0)
+            nc.gpsimd.tensor_copy(out=bias_sb[:], in_=bias_bf[:])
+            nc.scalar.activation(out=warm_out[:], in_=warm[:], func=ACT.Identity)
+
+            def copy(eng, out, in_):
+                if eng == "S":
+                    nc.scalar.copy(out, in_)
+                else:
+                    nc.vector.tensor_copy(out=out, in_=in_)
+
+            def transpose_rows(key, rows):
+                t = bank()
+                banks[key] = t
+                for r, row in enumerate(rows):
+                    words = row.bitcast(F32)
+                    for u in (0, 1):
+                        c = (len(rows) * u + r) * P
+                        nc.tensor.transpose(t[:, c : c + P], words[:, u::2], ident[:])
+
+            def cast_b(s, r, eng):
+                w = sb("wide%d%d" % (s, r), [P, 2 * D], BF16)
+                wide[s, r] = w[:, 0:D]
+                wide[s, r + 1] = w[:, D : 2 * D]
+                copy(eng, w[:], b_sb[s][:, r : r + 2, :].rearrange("p r d -> p (r d)").bitcast(FP8))
+
+            def t_b(s, r, n):
+                transpose_rows(("B", s, r), [wide[s, r + x] for x in range(n)])
+
+            def prod_b(s, r, n):
+                g = sb("gb%d%d" % (s, r), [P, n * 512], BF16)
+                grouped["B", s, r] = g
+                nc.vector.tensor_tensor(
+                    out=g[:].rearrange("p (c u e) -> p c u e", u=2, e=2),
+                    in0=banks["B", s, r][:, 0 : n * 256].bitcast(BF16).rearrange("p (u c e) -> p c u e", u=2, e=2),
+                    in1=scale_sb[:].unsqueeze(1).to_broadcast([P, n * P, 4]).rearrange("p c (u e) -> p c u e", u=2),
+                    op=ALU.mult,
+                )
+
+            def quant(codes, scales, g):
+                nc.vector.quantize_mx(out=codes.bitcast(FP8X4), scales=scales, in_=g)
+
+            def q_b(s, r, n):
+                c = sb("bc%d%d" % (s, r), [P, n * P], U32)
+                z = sb("bs%d%d" % (s, r), [P, n * P], U8)
+                quant(c[:], z[:], grouped["B", s, r][:])
+                for x in range(n):
+                    b_codes[s, r + x] = c[:, x * P : (x + 1) * P]
+                    b_scales[s, r + x] = z[:, x * P : (x + 1) * P]
+
+            def t_k(h):
+                transpose_rows(("K", h), [k_sb[:, 2 * h, :], k_sb[:, 2 * h + 1, :]])
+
+            def cp_k(h, eng):
+                g = sb("gk%d" % h, [P, 1024], BF16)
+                grouped["K", h] = g
+                copy(
+                    eng,
+                    g[:].bitcast(F32).rearrange("p (c u) -> p c u", u=2),
+                    banks["K", h][:].rearrange("p (u c) -> p c u", u=2),
+                )
+
+            def q_k(h):
+                quant(k_codes[:, 256 * h : 256 * h + 256], k_scales[:, 256 * h : 256 * h + 256], grouped["K", h][:])
+
+            def t_a(s, g):
+                transpose_rows(("A", s, g), [a_sb[s][:, g, 0, :], a_sb[s][:, g, 1, :]])
+
+            def cp_a(s, g, eng):
+                t = sb("ga%d%d" % (s, g), [P, 1024], BF16)
+                grouped["A", s, g] = t
+                copy(
+                    eng,
+                    t[:].bitcast(F32).rearrange("p (m r u) -> p m r u", r=2, u=2),
+                    banks["A", s, g][:].rearrange("p (u r m) -> p m r u", u=2, r=2),
+                )
+
+            def q_a(s, g):
+                a_codes[s, g] = sb("ac%d%d" % (s, g), [P, 256], U32)
+                a_scales[s, g] = sb("as%d%d" % (s, g), [P, 256], U8)
+                quant(a_codes[s, g][:], a_scales[s, g][:], grouped["A", s, g][:])
+
+            def m1(s, g, h):
+                t = bank()
+                banks["Q", s, g, h] = t
+                cols = slice(h * P, (h + 1) * P)
+                for c in range(4):
+                    rows = slice(c * P, (c + 1) * P)
+                    nc.tensor.matmul_mx(
+                        out=t[:, rows],
+                        lhsT=k_codes[:, rows].bitcast(FP8X4),
+                        lhsT_scale=k_scales[:, rows],
+                        rhs=a_codes[s, g][:, cols].bitcast(FP8X4),
+                        rhs_scale=a_scales[s, g][:, cols],
+                        start=True,
+                        stop=True,
+                    )
+
+            def cp_q(s, g, h, eng):
+                if ("Q", s, g) not in grouped:
+                    grouped["Q", s, g] = sb("gq%d%d" % (s, g), [P, 1024], BF16)
+                copy(
+                    eng,
+                    grouped["Q", s, g][:, h * 512 : h * 512 + 512].rearrange("p (j t) -> p j t", t=4),
+                    banks["Q", s, g, h][:].rearrange("p (t j) -> p j t", t=4),
+                )
+
+            def q_q(s, g):
+                cols = slice(g * 256, g * 256 + 256)
+                quant(q_codes[s][:, cols], q_scales[s][:, cols], grouped["Q", s, g][:])
+
+            def m2(s, r, lo, hi):
+                t = bank()
+                banks["O", s, r, lo] = t
+                nc.tensor.matmul_mx(
+                    out=t[:, 0 : hi - lo],
+                    lhsT=b_codes[s, r].bitcast(FP8X4),
+                    lhsT_scale=b_scales[s, r],
+                    rhs=q_codes[s][:, lo:hi].bitcast(FP8X4),
+                    rhs_scale=q_scales[s][:, lo:hi],
+                    start=True,
+                    stop=True,
+                )
+
+            def ev(s, r, lo, hi, eng):
+                if (s, r // 2) not in outs:
+                    outs[s, r // 2] = sb("o%d%d" % (s, r), [P, 2, N], F32)
+                o = outs[s, r // 2][:, r % 2, lo:hi]
+                t = banks["O", s, r, lo][:, 0 : hi - lo]
+                if eng == "S":
+                    nc.scalar.activation(out=o, in_=t, func=ACT.Identity, bias=bias_sb[:])
+                else:
+                    nc.vector.tensor_scalar(out=o, in0=t, scalar1=bias_sb[:], scalar2=None, op0=ALU.add)
+
+            def store(s, r, lo, hi):
+                nc.sync.dma_start(
+                    out=out_view[s, r][:, :, lo:hi],
+                    in_=outs[s, r // 2][:, r % 2, lo:hi].unsqueeze(1).to_broadcast([P, 2, hi - lo]),
+                )
+
+            def store_pair(s, r):
+                nc.sync.dma_start(
+                    out=pair_view[s, r // 2],
+                    in_=outs[s, r // 2][:].rearrange("p r j -> p (r j)").unsqueeze(1).to_broadcast([P, 2, 2 * N]),
+                )
+
+            steps = [
+                (t_k, 0),
+                (cast_b, 0, 0, "S"),
+                (cp_k, 0, "V"),
+                (q_k, 0),
+                (t_k, 1),
+                (cp_k, 1, "V"),
+                (cast_b, 0, 2, "V"),
+                (q_k, 1),
+                (t_a, 0, 0),
+                (t_b, 0, 0, 1),
+                (cp_a, 0, 0, "S"),
+                (q_a, 0, 0),
+                (t_b, 0, 1, 1),
+                (cast_b, 0, 6, "S"),
+                (t_a, 0, 1),
+                (cp_a, 0, 1, "S"),
+                (t_a, 0, 3),
+                (cp_a, 0, 3, "S"),
+                (m1, 0, 0, 1),
+                (cp_q, 0, 0, 1, "S"),
+                (t_b, 0, 2, 2),
+                (prod_b, 0, 0, 1),
+                (prod_b, 0, 1, 1),
+                (m1, 0, 0, 0),
+                (t_a, 0, 2),
+                (t_a, 1, 0),
+                (q_b, 0, 0, 1),
+                (q_a, 0, 1),
+                (m1, 0, 1, 1),
+                (prod_b, 0, 2, 2),
+                (cp_q, 0, 0, 0, "S"),
+                (cp_a, 0, 2, "S"),
+                (m1, 0, 1, 0),
+                (q_a, 0, 3),
+                (q_q, 0, 0),
+                (m1, 0, 3, 0),
+                (q_b, 0, 1, 1),
+                (q_b, 0, 2, 2),
+                (q_a, 0, 2),
+                (m2, 0, 0, 0, 256),
+                (cp_q, 0, 1, 1, "S"),
+                (ev, 0, 0, 0, 256, "V"),
+                (store, 0, 0, 0, 256),
+                (m2, 0, 1, 0, 256),
+                (cp_q, 0, 1, 0, "S"),
+                (q_q, 0, 1),
+                (cp_a, 1, 0, "S"),
+                (ev, 0, 1, 0, 256, "V"),
+                (store, 0, 1, 0, 256),
+                (cp_q, 0, 3, 0, "S"),
+                (m1, 0, 2, 0),
+                (cp_q, 0, 2, 0, "V"),
+                (cast_b, 0, 4, "V"),
+                (m1, 0, 3, 1),
+                (m2, 0, 1, 256, 512),
+                (ev, 0, 1, 256, 512, "S"),
+                (store, 0, 1, 256, 512),
+                (m2, 0, 3, 0, 512),
+                (ev, 0, 3, 0, 512, "S"),
+                (store, 0, 3, 0, 512),
+                (m1, 0, 2, 1),
+                (cp_q, 0, 2, 1, "S"),
+                (t_a, 1, 3),
+                (m2, 0, 0, 256, 512),
+                (cp_q, 0, 3, 1, "V"),
+                (q_q, 0, 3),
+                (m2, 0, 2, 0, 512),
+                (ev, 0, 0, 256, 512, "S"),
+                (store, 0, 0, 256, 512),
+                (t_b, 0, 4, 2),
+                (t_a, 1, 2),
+                (q_q, 0, 2),
+                (q_a, 1, 0),
+                (m2, 0, 3, 512, 1024),
+                (m2, 0, 0, 512, 1024),
+                (cast_b, 1, 6, "V"),
+                (ev, 0, 2, 0, 512, "S"),
+                (store, 0, 2, 0, 512),
+                (m2, 0, 1, 512, 1024),
+                (cp_a, 1, 3, "S"),
+                (ev, 0, 3, 512, 1024, "S"),
+                (store, 0, 3, 512, 1024),
+                (m2, 0, 2, 512, 1024),
+                (ev, 0, 1, 512, 1024, "S"),
+                (store, 0, 1, 512, 1024),
+                (ev, 0, 2, 512, 1024, "S"),
+                (store, 0, 2, 512, 1024),
+                (m1, 1, 0, 0),
+                (cp_q, 1, 0, 0, "S"),
+                (prod_b, 0, 4, 2),
+                (t_a, 1, 1),
+                (cp_a, 1, 2, "V"),
+                (t_b, 0, 6, 2),
+                (t_b, 1, 6, 2),
+                (q_b, 0, 4, 2),
+                (cp_a, 1, 1, "S"),
+                (ev, 0, 0, 512, 1024, "S"),
+                (store, 0, 0, 512, 1024),
+                (m2, 0, 5, 0, 512),
+                (ev, 0, 5, 0, 512, "S"),
+                (store, 0, 5, 0, 512),
+                (q_a, 1, 3),
+                (m2, 0, 4, 512, 1024),
+                (m2, 0, 4, 0, 512),
+                (ev, 0, 4, 0, 512, "S"),
+                (store, 0, 4, 0, 512),
+                (q_a, 1, 2),
+                (cast_b, 1, 4, "S"),
+                (prod_b, 0, 6, 2),
+                (m1, 1, 0, 1),
+                (m1, 1, 2, 0),
+                (cp_q, 1, 2, 0, "S"),
+                (q_a, 1, 1),
+                (m1, 1, 1, 0),
+                (prod_b, 1, 6, 2),
+                (q_b, 0, 6, 2),
+                (m1, 1, 1, 1),
+                (m2, 0, 5, 512, 1024),
+                (ev, 0, 5, 512, 1024, "S"),
+                (store, 0, 5, 512, 1024),
+                (cast_b, 1, 2, "V"),
+                (cp_q, 1, 1, 1, "S"),
+                (m2, 0, 7, 0, 512),
+                (ev, 0, 7, 0, 512, "S"),
+                (store, 0, 7, 0, 512),
+                (m2, 0, 6, 0, 512),
+                (m2, 0, 6, 512, 1024),
+                (ev, 0, 6, 512, 1024, "S"),
+                (store, 0, 6, 512, 1024),
+                (ev, 0, 4, 512, 1024, "V"),
+                (store, 0, 4, 512, 1024),
+                (cp_q, 1, 0, 1, "V"),
+                (ev, 0, 6, 0, 512, "S"),
+                (store, 0, 6, 0, 512),
+                (cp_q, 1, 1, 0, "V"),
+                (q_b, 1, 6, 2),
+                (m1, 1, 3, 1),
+                (t_b, 1, 2, 2),
+                (m1, 1, 2, 1),
+                (m2, 0, 7, 512, 1024),
+                (q_q, 1, 1),
+                (cast_b, 1, 0, "V"),
+                (m1, 1, 3, 0),
+                (t_b, 1, 4, 2),
+                (q_q, 1, 0),
+                (m2, 1, 6, 0, 512),
+                (prod_b, 1, 2, 2),
+                (q_b, 1, 2, 2),
+                (cp_q, 1, 2, 1, "S"),
+                (q_q, 1, 2),
+                (cp_q, 1, 3, 1, "S"),
+                (m2, 1, 7, 0, 512),
+                (cp_q, 1, 3, 0, "S"),
+                (q_q, 1, 3),
+                (m2, 1, 2, 512, 1024),
+                (m2, 1, 6, 512, 1024),
+                (prod_b, 1, 4, 2),
+                (ev, 0, 7, 512, 1024, "S"),
+                (store, 0, 7, 512, 1024),
+                (m2, 1, 7, 512, 1024),
+                (ev, 1, 7, 512, 1024, "V"),
+                (t_b, 1, 0, 2),
+                (prod_b, 1, 0, 2),
+                (ev, 1, 6, 0, 512, "S"),
+                (q_b, 1, 4, 2),
+                (m2, 1, 5, 512, 1024),
+                (ev, 1, 5, 512, 1024, "V"),
+                (m2, 1, 4, 512, 1024),
+                (ev, 1, 7, 0, 512, "S"),
+                (q_b, 1, 0, 2),
+                (m2, 1, 4, 0, 512),
+                (m2, 1, 5, 0, 512),
+                (m2, 1, 1, 0, 512),
+                (m2, 1, 3, 512, 1024),
+                (ev, 1, 6, 512, 1024, "S"),
+                (store_pair, 1, 6),
+                (m2, 1, 0, 512, 1024),
+                (ev, 1, 5, 0, 512, "S"),
+                (ev, 1, 4, 0, 512, "V"),
+                (ev, 1, 4, 512, 1024, "S"),
+                (store_pair, 1, 4),
+                (ev, 1, 1, 0, 512, "V"),
+                (ev, 1, 3, 512, 1024, "S"),
+                (m2, 1, 2, 0, 512),
+                (ev, 1, 2, 0, 512, "S"),
+                (m2, 1, 3, 0, 512),
+                (ev, 1, 3, 0, 512, "V"),
+                (ev, 1, 2, 512, 1024, "S"),
+                (store_pair, 1, 2),
+                (m2, 1, 0, 0, 512),
+                (m2, 1, 1, 512, 1024),
+                (ev, 1, 0, 0, 512, "V"),
+                (ev, 1, 1, 512, 1024, "S"),
+                (ev, 1, 0, 512, 1024, "V"),
+                (store_pair, 1, 0),
+            ]
+            for step in steps:
+                step[0](*step[1:])

@@ -211,200 +211,195 @@ def tile_bilinear_kernel(tc, tensor0, tensor1_bytes, tensor1_scale, kernel, bias
 
             steps = [
                 (t_k, 0),
-                (cast_b, 0, 0, "S"),
                 (cp_k, 0, "V"),
-                (q_k, 0),
                 (t_k, 1),
-                (cp_k, 1, "V"),
-                (cast_b, 0, 2, "V"),
-                (q_k, 1),
+                (cp_k, 1, "S"),
+                (cast_b, 0, 0, "V"),
                 (t_a, 0, 0),
-                (t_b, 0, 0, 1),
                 (cp_a, 0, 0, "S"),
-                (q_a, 0, 0),
-                (t_b, 0, 1, 1),
-                (cast_b, 0, 6, "S"),
                 (t_a, 0, 1),
+                (t_b, 0, 1, 1),
+                (t_b, 0, 0, 1),
+                (t_a, 0, 2),
                 (cp_a, 0, 1, "S"),
+                (cast_b, 0, 4, "S"),
+                (q_k, 0),
+                (q_k, 1),
                 (t_a, 0, 3),
                 (cp_a, 0, 3, "S"),
+                (q_a, 0, 0),
                 (m1, 0, 0, 1),
                 (cp_q, 0, 0, 1, "S"),
+                (m1, 0, 0, 0),
+                (cp_q, 0, 0, 0, "S"),
+                (prod_b, 0, 1, 1),
+                (cast_b, 0, 2, "V"),
+                (cp_a, 0, 2, "S"),
                 (t_b, 0, 2, 2),
                 (prod_b, 0, 0, 1),
-                (prod_b, 0, 1, 1),
-                (m1, 0, 0, 0),
-                (t_a, 0, 2),
-                (t_a, 1, 0),
-                (q_b, 0, 0, 1),
                 (q_a, 0, 1),
-                (m1, 0, 1, 1),
-                (prod_b, 0, 2, 2),
-                (cp_q, 0, 0, 0, "S"),
-                (cp_a, 0, 2, "S"),
                 (m1, 0, 1, 0),
-                (q_a, 0, 3),
-                (q_q, 0, 0),
-                (m1, 0, 3, 0),
-                (q_b, 0, 1, 1),
-                (q_b, 0, 2, 2),
-                (q_a, 0, 2),
-                (m2, 0, 0, 0, 256),
-                (cp_q, 0, 1, 1, "S"),
-                (ev, 0, 0, 0, 256, "V"),
-                (store, 0, 0, 0, 256),
-                (m2, 0, 1, 0, 256),
+                (cast_b, 0, 6, "V"),
                 (cp_q, 0, 1, 0, "S"),
+                (m1, 0, 1, 1),
+                (q_b, 0, 0, 1),
+                (q_b, 0, 1, 1),
+                (t_a, 1, 0),
+                (q_q, 0, 0),
+                (m2, 0, 1, 0, 256),
+                (q_a, 0, 3),
+                (cp_q, 0, 1, 1, "S"),
+                (m2, 0, 0, 0, 256),
+                (ev, 0, 0, 0, 256, "S"),
+                (store, 0, 0, 0, 256),
+                (m1, 0, 3, 0),
+                (t_b, 0, 4, 2),
+                (prod_b, 0, 2, 2),
                 (q_q, 0, 1),
-                (cp_a, 1, 0, "S"),
-                (ev, 0, 1, 0, 256, "V"),
+                (ev, 0, 1, 0, 256, "S"),
                 (store, 0, 1, 0, 256),
-                (cp_q, 0, 3, 0, "S"),
-                (m1, 0, 2, 0),
-                (cp_q, 0, 2, 0, "V"),
-                (cast_b, 0, 4, "V"),
                 (m1, 0, 3, 1),
+                (cp_q, 0, 3, 0, "S"),
                 (m2, 0, 1, 256, 512),
+                (m2, 0, 0, 256, 512),
                 (ev, 0, 1, 256, 512, "S"),
                 (store, 0, 1, 256, 512),
-                (m2, 0, 3, 0, 512),
-                (ev, 0, 3, 0, 512, "S"),
-                (store, 0, 3, 0, 512),
-                (m1, 0, 2, 1),
-                (cp_q, 0, 2, 1, "S"),
-                (t_a, 1, 3),
-                (m2, 0, 0, 256, 512),
-                (cp_q, 0, 3, 1, "V"),
-                (q_q, 0, 3),
+                (q_b, 0, 2, 2),
                 (m2, 0, 2, 0, 512),
+                (q_a, 0, 2),
+                (m1, 0, 2, 1),
                 (ev, 0, 0, 256, 512, "S"),
                 (store, 0, 0, 256, 512),
-                (t_b, 0, 4, 2),
-                (t_a, 1, 2),
-                (q_q, 0, 2),
-                (q_a, 1, 0),
-                (m2, 0, 3, 512, 1024),
-                (m2, 0, 0, 512, 1024),
-                (cast_b, 1, 6, "V"),
+                (prod_b, 0, 4, 2),
                 (ev, 0, 2, 0, 512, "S"),
                 (store, 0, 2, 0, 512),
-                (m2, 0, 1, 512, 1024),
+                (m1, 0, 2, 0),
+                (cp_q, 0, 2, 0, "S"),
+                (cp_q, 0, 3, 1, "V"),
+                (m2, 0, 3, 0, 512),
+                (cp_q, 0, 2, 1, "V"),
+                (q_q, 0, 3),
+                (ev, 0, 3, 0, 512, "S"),
+                (store, 0, 3, 0, 512),
+                (t_a, 1, 3),
                 (cp_a, 1, 3, "S"),
+                (t_b, 0, 6, 2),
+                (q_q, 0, 2),
+                (m2, 0, 3, 512, 1024),
+                (cp_a, 1, 0, "S"),
+                (cast_b, 1, 2, "V"),
+                (m2, 0, 1, 512, 1024),
                 (ev, 0, 3, 512, 1024, "S"),
                 (store, 0, 3, 512, 1024),
-                (m2, 0, 2, 512, 1024),
-                (ev, 0, 1, 512, 1024, "S"),
+                (q_a, 1, 3),
+                (m1, 1, 3, 0),
+                (cast_b, 1, 6, "V"),
+                (t_a, 1, 2),
+                (cp_q, 1, 3, 0, "S"),
+                (ev, 0, 1, 512, 1024, "V"),
                 (store, 0, 1, 512, 1024),
-                (ev, 0, 2, 512, 1024, "S"),
-                (store, 0, 2, 512, 1024),
-                (m1, 1, 0, 0),
-                (cp_q, 1, 0, 0, "S"),
-                (prod_b, 0, 4, 2),
-                (t_a, 1, 1),
-                (cp_a, 1, 2, "V"),
-                (t_b, 0, 6, 2),
-                (t_b, 1, 6, 2),
-                (q_b, 0, 4, 2),
-                (cp_a, 1, 1, "S"),
+                (cp_a, 1, 2, "S"),
+                (m2, 0, 0, 512, 1024),
                 (ev, 0, 0, 512, 1024, "S"),
                 (store, 0, 0, 512, 1024),
-                (m2, 0, 5, 0, 512),
-                (ev, 0, 5, 0, 512, "S"),
-                (store, 0, 5, 0, 512),
-                (q_a, 1, 3),
-                (m2, 0, 4, 512, 1024),
+                (m1, 1, 3, 1),
+                (q_b, 0, 4, 2),
+                (m2, 0, 5, 512, 1024),
                 (m2, 0, 4, 0, 512),
                 (ev, 0, 4, 0, 512, "S"),
-                (store, 0, 4, 0, 512),
-                (q_a, 1, 2),
-                (cast_b, 1, 4, "S"),
-                (prod_b, 0, 6, 2),
-                (m1, 1, 0, 1),
-                (m1, 1, 2, 0),
-                (cp_q, 1, 2, 0, "S"),
-                (q_a, 1, 1),
-                (m1, 1, 1, 0),
-                (prod_b, 1, 6, 2),
-                (q_b, 0, 6, 2),
-                (m1, 1, 1, 1),
-                (m2, 0, 5, 512, 1024),
-                (ev, 0, 5, 512, 1024, "S"),
-                (store, 0, 5, 512, 1024),
-                (cast_b, 1, 2, "V"),
-                (cp_q, 1, 1, 1, "S"),
-                (m2, 0, 7, 0, 512),
-                (ev, 0, 7, 0, 512, "S"),
-                (store, 0, 7, 0, 512),
-                (m2, 0, 6, 0, 512),
-                (m2, 0, 6, 512, 1024),
-                (ev, 0, 6, 512, 1024, "S"),
-                (store, 0, 6, 512, 1024),
-                (ev, 0, 4, 512, 1024, "V"),
-                (store, 0, 4, 512, 1024),
-                (cp_q, 1, 0, 1, "V"),
-                (ev, 0, 6, 0, 512, "S"),
-                (store, 0, 6, 0, 512),
-                (cp_q, 1, 1, 0, "V"),
-                (q_b, 1, 6, 2),
-                (m1, 1, 3, 1),
-                (t_b, 1, 2, 2),
-                (m1, 1, 2, 1),
-                (m2, 0, 7, 512, 1024),
-                (q_q, 1, 1),
-                (cast_b, 1, 0, "V"),
-                (m1, 1, 3, 0),
-                (t_b, 1, 4, 2),
-                (q_q, 1, 0),
-                (m2, 1, 6, 0, 512),
-                (prod_b, 1, 2, 2),
-                (q_b, 1, 2, 2),
-                (cp_q, 1, 2, 1, "S"),
-                (q_q, 1, 2),
                 (cp_q, 1, 3, 1, "S"),
-                (m2, 1, 7, 0, 512),
-                (cp_q, 1, 3, 0, "S"),
-                (q_q, 1, 3),
-                (m2, 1, 2, 512, 1024),
-                (m2, 1, 6, 512, 1024),
-                (prod_b, 1, 4, 2),
-                (ev, 0, 7, 512, 1024, "S"),
-                (store, 0, 7, 512, 1024),
-                (m2, 1, 7, 512, 1024),
-                (ev, 1, 7, 512, 1024, "V"),
+                (q_a, 1, 0),
+                (m1, 1, 0, 0),
+                (m2, 0, 2, 512, 1024),
+                (cast_b, 1, 0, "V"),
+                (prod_b, 0, 6, 2),
                 (t_b, 1, 0, 2),
+                (cp_q, 1, 0, 0, "S"),
+                (ev, 0, 2, 512, 1024, "V"),
+                (store, 0, 2, 512, 1024),
+                (ev, 0, 5, 512, 1024, "S"),
+                (t_b, 1, 6, 2),
+                (m2, 0, 5, 0, 512),
+                (ev, 0, 5, 0, 512, "S"),
+                (store, 0, 5, 0, 1024),
+                (q_b, 0, 6, 2),
+                (m2, 0, 6, 0, 512),
+                (q_a, 1, 2),
+                (m1, 1, 2, 1),
+                (t_a, 1, 1),
+                (prod_b, 1, 6, 2),
+                (m2, 0, 7, 512, 1024),
+                (cp_a, 1, 1, "S"),
                 (prod_b, 1, 0, 2),
-                (ev, 1, 6, 0, 512, "S"),
-                (q_b, 1, 4, 2),
-                (m2, 1, 5, 512, 1024),
-                (ev, 1, 5, 512, 1024, "V"),
-                (m2, 1, 4, 512, 1024),
-                (ev, 1, 7, 0, 512, "S"),
+                (q_a, 1, 1),
+                (m2, 0, 4, 512, 1024),
+                (ev, 0, 4, 512, 1024, "S"),
+                (store, 0, 4, 0, 1024),
+                (m2, 0, 6, 512, 1024),
+                (ev, 0, 7, 512, 1024, "S"),
+                (m1, 1, 2, 0),
+                (cp_q, 1, 2, 1, "V"),
+                (m1, 1, 1, 0),
                 (q_b, 1, 0, 2),
-                (m2, 1, 4, 0, 512),
-                (m2, 1, 5, 0, 512),
-                (m2, 1, 1, 0, 512),
-                (m2, 1, 3, 512, 1024),
-                (ev, 1, 6, 512, 1024, "S"),
-                (store_pair, 1, 6),
+                (cp_q, 1, 1, 0, "S"),
+                (m2, 0, 7, 0, 512),
+                (ev, 0, 6, 0, 512, "S"),
+                (cp_q, 1, 2, 0, "S"),
+                (m1, 1, 0, 1),
+                (t_b, 1, 2, 2),
+                (ev, 0, 6, 512, 1024, "V"),
+                (q_b, 1, 6, 2),
+                (m1, 1, 1, 1),
+                (q_q, 1, 3),
+                (cp_q, 1, 0, 1, "S"),
+                (ev, 0, 7, 0, 512, "V"),
+                (store_pair, 0, 6),
+                (cp_q, 1, 1, 1, "S"),
+                (prod_b, 1, 2, 2),
+                (q_q, 1, 2),
                 (m2, 1, 0, 512, 1024),
-                (ev, 1, 5, 0, 512, "S"),
-                (ev, 1, 4, 0, 512, "V"),
-                (ev, 1, 4, 512, 1024, "S"),
-                (store_pair, 1, 4),
-                (ev, 1, 1, 0, 512, "V"),
-                (ev, 1, 3, 512, 1024, "S"),
-                (m2, 1, 2, 0, 512),
-                (ev, 1, 2, 0, 512, "S"),
+                (m2, 1, 1, 512, 1024),
+                (q_q, 1, 1),
+                (q_q, 1, 0),
+                (m2, 1, 0, 0, 512),
+                (ev, 1, 0, 0, 512, "S"),
+                (m2, 1, 1, 0, 512),
+                (cast_b, 1, 4, "V"),
+                (t_b, 1, 4, 2),
+                (q_b, 1, 2, 2),
+                (m2, 1, 3, 512, 1024),
+                (ev, 1, 1, 512, 1024, "V"),
                 (m2, 1, 3, 0, 512),
                 (ev, 1, 3, 0, 512, "V"),
-                (ev, 1, 2, 512, 1024, "S"),
-                (store_pair, 1, 2),
-                (m2, 1, 0, 0, 512),
-                (m2, 1, 1, 512, 1024),
-                (ev, 1, 0, 0, 512, "V"),
-                (ev, 1, 1, 512, 1024, "S"),
-                (ev, 1, 0, 512, 1024, "V"),
+                (prod_b, 1, 4, 2),
+                (ev, 1, 0, 512, 1024, "S"),
+                (m2, 1, 7, 0, 512),
+                (ev, 1, 7, 0, 512, "V"),
+                (m2, 1, 6, 0, 512),
+                (m2, 1, 2, 0, 512),
+                (ev, 1, 1, 0, 512, "S"),
                 (store_pair, 1, 0),
+                (m2, 1, 2, 512, 1024),
+                (ev, 1, 2, 0, 512, "S"),
+                (m2, 1, 6, 512, 1024),
+                (q_b, 1, 4, 2),
+                (m2, 1, 4, 512, 1024),
+                (m2, 1, 5, 0, 512),
+                (m2, 1, 5, 512, 1024),
+                (ev, 1, 4, 512, 1024, "V"),
+                (ev, 1, 3, 512, 1024, "S"),
+                (ev, 1, 2, 512, 1024, "V"),
+                (store_pair, 1, 2),
+                (m2, 1, 4, 0, 512),
+                (ev, 1, 5, 0, 512, "V"),
+                (ev, 1, 5, 512, 1024, "V"),
+                (ev, 1, 4, 0, 512, "V"),
+                (store_pair, 1, 4),
+                (m2, 1, 7, 512, 1024),
+                (ev, 1, 6, 512, 1024, "V"),
+                (ev, 1, 7, 512, 1024, "S"),
+                (ev, 1, 6, 0, 512, "S"),
+                (store_pair, 1, 6),
             ]
             for step in steps:
                 step[0](*step[1:])

@@ -35,6 +35,7 @@ def tile_bilinear_kernel(tc, tensor0, tensor1_bytes, tensor1_scale, kernel, bias
         bias_sb = sb("bias_sb", [P, 1], F32)
         warm = sb("warm", [P, 1], F32)
         warm_out = sb("warm_out", [P, 1], F32)
+        dummy = sb("dummy", [P, 512], BF16)
         k_sb = sb("k_sb", [P, 4, D], BF16)
         a_sb = [sb("a_sb%d" % s, [P, 4, 2, D], BF16) for s in range(S)]
         b_sb = [sb("b_sb%d" % s, [P, 8, D], U8) for s in range(S)]
@@ -51,18 +52,19 @@ def tile_bilinear_kernel(tc, tensor0, tensor1_bytes, tensor1_scale, kernel, bias
         out_view = out.rearrange("b s (p r) j -> s r p b j", r=8)
 
         with tc.manual_schedule():
-            nc.scalar.dma_start(out=scale_sb[:], in_=tensor1_scale.rearrange("a b (p t) -> p (a b t)", t=4))
-            nc.scalar.dma_start(out=bias_bf[:], in_=bias.partition_broadcast(P))
             k_in = kernel.rearrange("(p t) e -> p t e", t=4)
             nc.sync.dma_start(out=k_sb[:, 0:2, :], in_=k_in[:, 0:2, :])
             nc.sync.dma_start(out=k_sb[:, 2:4, :], in_=k_in[:, 2:4, :])
             nc.sync.dma_start(out=a_sb[0][:, 0], in_=a_in[0][:, 0])
             nc.sync.dma_start(out=b_sb[0][:, 0:2, :], in_=b_in[0][:, 0:2, :])
+            nc.sync.dma_start(out=scale_sb[:], in_=tensor1_scale.rearrange("a b (p t) -> p (a b t)", t=4))
             nc.sync.dma_start(out=a_sb[0][:, 1], in_=a_in[0][:, 1])
+            nc.sync.dma_start(out=bias_bf[:], in_=bias.partition_broadcast(P))
             nc.sync.dma_start(out=b_sb[0][:, 2:8, :], in_=b_in[0][:, 2:8, :])
             nc.sync.dma_start(out=a_sb[0][:, 2:4], in_=a_in[0][:, 2:4])
             nc.sync.dma_start(out=a_sb[1][:], in_=a_in[1])
             nc.sync.dma_start(out=b_sb[1][:], in_=b_in[1])
+            nc.vector.memset(dummy[:], 0.0)
             make_identity(nc, ident[:])
             nc.gpsimd.memset(warm[:], 0.0)
             nc.gpsimd.tensor_copy(out=bias_sb[:], in_=bias_bf[:])
@@ -73,6 +75,11 @@ def tile_bilinear_kernel(tc, tensor0, tensor1_bytes, tensor1_scale, kernel, bias
                     nc.scalar.copy(out, in_)
                 else:
                     nc.vector.tensor_copy(out=out, in_=in_)
+
+            def spin(n):
+                t = bank()
+                for x in range(n):
+                    nc.tensor.matmul(t[:], lhsT=dummy[:, 0:P], rhs=dummy[:], start=True, stop=True)
 
             def transpose_rows(key, rows):
                 t = bank()
@@ -210,196 +217,200 @@ def tile_bilinear_kernel(tc, tensor0, tensor1_bytes, tensor1_scale, kernel, bias
                 )
 
             steps = [
+                (spin, 5),
                 (t_k, 0),
                 (cp_k, 0, "V"),
+                (q_k, 0),
                 (t_k, 1),
-                (cp_k, 1, "S"),
+                (spin, 1),
                 (cast_b, 0, 0, "V"),
                 (t_a, 0, 0),
-                (cp_a, 0, 0, "S"),
-                (t_a, 0, 1),
-                (t_b, 0, 1, 1),
-                (t_b, 0, 0, 1),
-                (t_a, 0, 2),
-                (cp_a, 0, 1, "S"),
-                (cast_b, 0, 4, "S"),
-                (q_k, 0),
+                (spin, 1),
+                (cp_k, 1, "S"),
                 (q_k, 1),
-                (t_a, 0, 3),
-                (cp_a, 0, 3, "S"),
+                (cp_a, 0, 0, "S"),
                 (q_a, 0, 0),
-                (m1, 0, 0, 1),
-                (cp_q, 0, 0, 1, "S"),
-                (m1, 0, 0, 0),
-                (cp_q, 0, 0, 0, "S"),
-                (prod_b, 0, 1, 1),
-                (cast_b, 0, 2, "V"),
-                (cp_a, 0, 2, "S"),
-                (t_b, 0, 2, 2),
+                (cast_b, 0, 6, "V"),
+                (t_a, 0, 1),
+                (cp_a, 0, 1, "S"),
+                (t_b, 0, 0, 1),
+                (cast_b, 0, 2, "S"),
                 (prod_b, 0, 0, 1),
                 (q_a, 0, 1),
-                (m1, 0, 1, 0),
-                (cast_b, 0, 6, "V"),
-                (cp_q, 0, 1, 0, "S"),
-                (m1, 0, 1, 1),
-                (q_b, 0, 0, 1),
+                (t_b, 0, 1, 1),
+                (spin, 1),
+                (prod_b, 0, 1, 1),
                 (q_b, 0, 1, 1),
-                (t_a, 1, 0),
+                (m1, 0, 0, 1),
+                (m1, 0, 0, 0),
+                (t_a, 0, 2),
+                (cp_q, 0, 0, 1, "S"),
+                (q_b, 0, 0, 1),
+                (t_b, 0, 2, 2),
+                (prod_b, 0, 2, 2),
+                (cp_q, 0, 0, 0, "S"),
+                (t_a, 0, 3),
+                (cp_a, 0, 2, "S"),
+                (cp_a, 0, 3, "S"),
+                (m1, 0, 1, 0),
+                (cp_q, 0, 1, 0, "S"),
                 (q_q, 0, 0),
-                (m2, 0, 1, 0, 256),
-                (q_a, 0, 3),
+                (m1, 0, 1, 1),
                 (cp_q, 0, 1, 1, "S"),
                 (m2, 0, 0, 0, 256),
+                (q_a, 0, 3),
+                (m1, 0, 3, 1),
                 (ev, 0, 0, 0, 256, "S"),
                 (store, 0, 0, 0, 256),
-                (m1, 0, 3, 0),
-                (t_b, 0, 4, 2),
-                (prod_b, 0, 2, 2),
-                (q_q, 0, 1),
+                (m2, 0, 1, 0, 256),
                 (ev, 0, 1, 0, 256, "S"),
                 (store, 0, 1, 0, 256),
-                (m1, 0, 3, 1),
-                (cp_q, 0, 3, 0, "S"),
-                (m2, 0, 1, 256, 512),
-                (m2, 0, 0, 256, 512),
-                (ev, 0, 1, 256, 512, "S"),
-                (store, 0, 1, 256, 512),
-                (q_b, 0, 2, 2),
-                (m2, 0, 2, 0, 512),
                 (q_a, 0, 2),
-                (m1, 0, 2, 1),
-                (ev, 0, 0, 256, 512, "S"),
-                (store, 0, 0, 256, 512),
-                (prod_b, 0, 4, 2),
-                (ev, 0, 2, 0, 512, "S"),
-                (store, 0, 2, 0, 512),
                 (m1, 0, 2, 0),
                 (cp_q, 0, 2, 0, "S"),
-                (cp_q, 0, 3, 1, "V"),
+                (q_b, 0, 2, 2),
+                (q_q, 0, 1),
+                (m1, 0, 3, 0),
+                (m2, 0, 1, 256, 512),
+                (ev, 0, 1, 256, 512, "S"),
+                (store, 0, 1, 256, 512),
+                (m2, 0, 0, 256, 512),
+                (ev, 0, 0, 256, 512, "S"),
+                (store, 0, 0, 256, 512),
+                (m1, 0, 2, 1),
                 (m2, 0, 3, 0, 512),
-                (cp_q, 0, 2, 1, "V"),
-                (q_q, 0, 3),
+                (m2, 0, 2, 0, 512),
+                (ev, 0, 2, 0, 512, "S"),
+                (store, 0, 2, 0, 512),
                 (ev, 0, 3, 0, 512, "S"),
                 (store, 0, 3, 0, 512),
-                (t_a, 1, 3),
-                (cp_a, 1, 3, "S"),
-                (t_b, 0, 6, 2),
-                (q_q, 0, 2),
-                (m2, 0, 3, 512, 1024),
-                (cp_a, 1, 0, "S"),
-                (cast_b, 1, 2, "V"),
-                (m2, 0, 1, 512, 1024),
-                (ev, 0, 3, 512, 1024, "S"),
-                (store, 0, 3, 512, 1024),
-                (q_a, 1, 3),
-                (m1, 1, 3, 0),
-                (cast_b, 1, 6, "V"),
+                (cp_q, 0, 3, 1, "V"),
+                (t_a, 1, 1),
+                (cp_a, 1, 1, "S"),
+                (cast_b, 0, 4, "V"),
+                (cp_q, 0, 3, 0, "V"),
+                (cp_q, 0, 2, 1, "V"),
+                (t_b, 0, 4, 2),
                 (t_a, 1, 2),
-                (cp_q, 1, 3, 0, "S"),
+                (t_a, 1, 3),
+                (q_q, 0, 3),
+                (q_q, 0, 2),
+                (prod_b, 0, 4, 2),
+                (q_b, 0, 4, 2),
+                (m2, 0, 0, 512, 1024),
+                (ev, 0, 0, 512, 1024, "V"),
+                (store, 0, 0, 512, 1024),
+                (cp_a, 1, 3, "S"),
+                (cast_b, 1, 6, "S"),
+                (cast_b, 1, 0, "S"),
+                (q_a, 1, 3),
+                (m2, 0, 1, 512, 1024),
                 (ev, 0, 1, 512, 1024, "V"),
                 (store, 0, 1, 512, 1024),
-                (cp_a, 1, 2, "S"),
-                (m2, 0, 0, 512, 1024),
-                (ev, 0, 0, 512, 1024, "S"),
-                (store, 0, 0, 512, 1024),
-                (m1, 1, 3, 1),
-                (q_b, 0, 4, 2),
-                (m2, 0, 5, 512, 1024),
-                (m2, 0, 4, 0, 512),
-                (ev, 0, 4, 0, 512, "S"),
-                (cp_q, 1, 3, 1, "S"),
-                (q_a, 1, 0),
-                (m1, 1, 0, 0),
                 (m2, 0, 2, 512, 1024),
-                (cast_b, 1, 0, "V"),
-                (prod_b, 0, 6, 2),
-                (t_b, 1, 0, 2),
-                (cp_q, 1, 0, 0, "S"),
+                (t_a, 1, 0),
+                (cp_a, 1, 0, "V"),
+                (m2, 0, 3, 512, 1024),
+                (m1, 1, 3, 1),
+                (ev, 0, 3, 512, 1024, "S"),
+                (store, 0, 3, 512, 1024),
+                (m2, 0, 5, 0, 512),
+                (q_a, 1, 0),
                 (ev, 0, 2, 512, 1024, "V"),
                 (store, 0, 2, 512, 1024),
-                (ev, 0, 5, 512, 1024, "S"),
-                (t_b, 1, 6, 2),
-                (m2, 0, 5, 0, 512),
-                (ev, 0, 5, 0, 512, "S"),
-                (store, 0, 5, 0, 1024),
-                (q_b, 0, 6, 2),
-                (m2, 0, 6, 0, 512),
-                (q_a, 1, 2),
-                (m1, 1, 2, 1),
-                (t_a, 1, 1),
-                (prod_b, 1, 6, 2),
-                (m2, 0, 7, 512, 1024),
-                (cp_a, 1, 1, "S"),
-                (prod_b, 1, 0, 2),
                 (q_a, 1, 1),
                 (m2, 0, 4, 512, 1024),
+                (m2, 0, 5, 512, 1024),
+                (t_b, 0, 6, 2),
+                (prod_b, 0, 6, 2),
+                (q_b, 0, 6, 2),
+                (cp_q, 1, 3, 1, "S"),
+                (ev, 0, 5, 512, 1024, "S"),
+                (cp_a, 1, 2, "S"),
+                (t_b, 1, 6, 2),
+                (q_a, 1, 2),
+                (m1, 1, 1, 1),
+                (m1, 1, 0, 1),
+                (m1, 1, 3, 0),
+                (cast_b, 1, 2, "V"),
+                (m1, 1, 0, 0),
+                (ev, 0, 5, 0, 512, "S"),
+                (store, 0, 5, 0, 1024),
+                (cast_b, 1, 4, "V"),
+                (cp_q, 1, 0, 1, "S"),
+                (cp_q, 1, 1, 1, "S"),
+                (m1, 1, 1, 0),
+                (m1, 1, 2, 0),
+                (cp_q, 1, 1, 0, "S"),
+                (cp_q, 1, 3, 0, "S"),
+                (m2, 0, 4, 0, 512),
+                (ev, 0, 4, 0, 512, "V"),
+                (t_b, 1, 2, 2),
+                (m2, 0, 7, 512, 1024),
+                (prod_b, 1, 2, 2),
                 (ev, 0, 4, 512, 1024, "S"),
                 (store, 0, 4, 0, 1024),
-                (m2, 0, 6, 512, 1024),
-                (ev, 0, 7, 512, 1024, "S"),
-                (m1, 1, 2, 0),
-                (cp_q, 1, 2, 1, "V"),
-                (m1, 1, 1, 0),
-                (q_b, 1, 0, 2),
-                (cp_q, 1, 1, 0, "S"),
-                (m2, 0, 7, 0, 512),
-                (ev, 0, 6, 0, 512, "S"),
                 (cp_q, 1, 2, 0, "S"),
-                (m1, 1, 0, 1),
-                (t_b, 1, 2, 2),
-                (ev, 0, 6, 512, 1024, "V"),
-                (q_b, 1, 6, 2),
-                (m1, 1, 1, 1),
-                (q_q, 1, 3),
-                (cp_q, 1, 0, 1, "S"),
-                (ev, 0, 7, 0, 512, "V"),
-                (store_pair, 0, 6),
-                (cp_q, 1, 1, 1, "S"),
-                (prod_b, 1, 2, 2),
-                (q_q, 1, 2),
-                (m2, 1, 0, 512, 1024),
-                (m2, 1, 1, 512, 1024),
-                (q_q, 1, 1),
-                (q_q, 1, 0),
-                (m2, 1, 0, 0, 512),
-                (ev, 1, 0, 0, 512, "S"),
-                (m2, 1, 1, 0, 512),
-                (cast_b, 1, 4, "V"),
-                (t_b, 1, 4, 2),
                 (q_b, 1, 2, 2),
-                (m2, 1, 3, 512, 1024),
-                (ev, 1, 1, 512, 1024, "V"),
-                (m2, 1, 3, 0, 512),
-                (ev, 1, 3, 0, 512, "V"),
-                (prod_b, 1, 4, 2),
-                (ev, 1, 0, 512, 1024, "S"),
-                (m2, 1, 7, 0, 512),
-                (ev, 1, 7, 0, 512, "V"),
-                (m2, 1, 6, 0, 512),
+                (m2, 0, 6, 512, 1024),
+                (ev, 0, 6, 512, 1024, "V"),
+                (m2, 0, 6, 0, 512),
+                (ev, 0, 7, 512, 1024, "S"),
+                (t_b, 1, 4, 2),
+                (ev, 0, 6, 0, 512, "V"),
+                (q_q, 1, 3),
+                (q_q, 1, 1),
+                (m2, 0, 7, 0, 512),
+                (ev, 0, 7, 0, 512, "S"),
+                (store_pair, 0, 6),
+                (m1, 1, 2, 1),
+                (cp_q, 1, 0, 0, "S"),
+                (q_q, 1, 0),
+                (cp_q, 1, 2, 1, "S"),
+                (t_b, 1, 0, 2),
+                (prod_b, 1, 0, 2),
+                (q_q, 1, 2),
                 (m2, 1, 2, 0, 512),
-                (ev, 1, 1, 0, 512, "S"),
-                (store_pair, 1, 0),
-                (m2, 1, 2, 512, 1024),
                 (ev, 1, 2, 0, 512, "S"),
-                (m2, 1, 6, 512, 1024),
-                (q_b, 1, 4, 2),
-                (m2, 1, 4, 512, 1024),
-                (m2, 1, 5, 0, 512),
-                (m2, 1, 5, 512, 1024),
-                (ev, 1, 4, 512, 1024, "V"),
-                (ev, 1, 3, 512, 1024, "S"),
+                (q_b, 1, 0, 2),
+                (m2, 1, 3, 0, 512),
+                (ev, 1, 3, 0, 512, "S"),
+                (m2, 1, 3, 512, 1024),
+                (m2, 1, 2, 512, 1024),
                 (ev, 1, 2, 512, 1024, "V"),
+                (prod_b, 1, 6, 2),
+                (q_b, 1, 6, 2),
+                (ev, 1, 3, 512, 1024, "S"),
                 (store_pair, 1, 2),
-                (m2, 1, 4, 0, 512),
-                (ev, 1, 5, 0, 512, "V"),
-                (ev, 1, 5, 512, 1024, "V"),
-                (ev, 1, 4, 0, 512, "V"),
-                (store_pair, 1, 4),
+                (m2, 1, 1, 512, 1024),
+                (m2, 1, 0, 0, 512),
+                (prod_b, 1, 4, 2),
+                (m2, 1, 7, 0, 512),
+                (ev, 1, 7, 0, 512, "S"),
+                (q_b, 1, 4, 2),
                 (m2, 1, 7, 512, 1024),
-                (ev, 1, 6, 512, 1024, "V"),
                 (ev, 1, 7, 512, 1024, "S"),
-                (ev, 1, 6, 0, 512, "S"),
+                (m2, 1, 6, 0, 512),
+                (ev, 1, 6, 0, 512, "V"),
+                (m2, 1, 0, 512, 1024),
+                (m2, 1, 6, 512, 1024),
+                (ev, 1, 6, 512, 1024, "S"),
                 (store_pair, 1, 6),
+                (ev, 1, 0, 512, 1024, "S"),
+                (m2, 1, 5, 0, 512),
+                (ev, 1, 1, 512, 1024, "V"),
+                (ev, 1, 5, 0, 512, "S"),
+                (m2, 1, 1, 0, 512),
+                (m2, 1, 4, 512, 1024),
+                (ev, 1, 4, 512, 1024, "S"),
+                (ev, 1, 1, 0, 512, "S"),
+                (m2, 1, 4, 0, 512),
+                (ev, 1, 4, 0, 512, "V"),
+                (m2, 1, 5, 512, 1024),
+                (ev, 1, 5, 512, 1024, "V"),
+                (store_pair, 1, 4),
+                (ev, 1, 0, 0, 512, "S"),
+                (store_pair, 1, 0),
             ]
             for step in steps:
                 step[0](*step[1:])

@@ -9,408 +9,360 @@ U32 = mybir.dt.uint32
 U8 = mybir.dt.uint8
 FP8 = mybir.dt.float8_e4m3fn
 FP8X4 = mybir.dt.float8_e4m3fn_x4
-ACT = mybir.ActivationFunctionType
-ALU = mybir.AluOpType
+IDENTITY = mybir.ActivationFunctionType.Identity
+ADD = mybir.AluOpType.add
+MULT = mybir.AluOpType.mult
 
 P = 128
-S, N, D = 2, 1024, 512
+COPIES, S, N, D = 2, 2, 1024, 512
+PACK = 4
+BANK = 512
+GROUP = 256
+ROW_TILES = N // P
+HALF = N // 2
+
 FLOPS = 2 * S * N * D * D + 2 * S * N * N * D
 
 
 def tile_bilinear_kernel(tc, tensor0, tensor1_bytes, tensor1_scale, kernel, bias, out):
     nc = tc.nc
+
     with ExitStack() as ctx:
         keep = ctx.enter_context(tc.tile_pool(name="keep", bufs=1))
         psum = ctx.enter_context(tc.psum_pool(name="psum", bufs=8))
+        ctx.enter_context(tc.manual_schedule())
 
-        def sb(name, shape, dtype):
+        def sbuf(name, shape, dtype):
             return keep.tile(shape, dtype, name=name, align_bytes=64)
 
-        def bank():
-            return psum.tile([P, 512], F32, name="bank")
+        def psum_bank():
+            return psum.tile([P, BANK], F32, name="bank")
 
-        ident = sb("ident", [P, P], F32)
-        scale_sb = sb("scale_sb", [P, 4], F32)
-        bias_bf = sb("bias_bf", [P, 1], BF16)
-        bias_sb = sb("bias_sb", [P, 1], F32)
-        warm = sb("warm", [P, 1], F32)
-        warm_out = sb("warm_out", [P, 1], F32)
-        dummy = sb("dummy", [P, 512], BF16)
-        k_sb = sb("k_sb", [P, 4, D], BF16)
-        a_sb = [sb("a_sb%d" % s, [P, 4, 2, D], BF16) for s in range(S)]
-        b_sb = [sb("b_sb%d" % s, [P, 8, D], U8) for s in range(S)]
-        k_codes = sb("k_codes", [P, D], U32)
-        k_scales = sb("k_scales", [P, D], U8)
-        q_codes = [sb("q_codes%d" % s, [P, N], U32) for s in range(S)]
-        q_scales = [sb("q_scales%d" % s, [P, N], U8) for s in range(S)]
-        a_codes, a_scales, b_codes, b_scales = {}, {}, {}, {}
-        banks, grouped, wide, outs = {}, {}, {}, {}
+        kernel_sb = sbuf("kernel_sb", [P, PACK, D], BF16)
+        tensor0_sb = [sbuf("tensor0_sb%d" % s, [P, N // GROUP, 2, D], BF16) for s in range(S)]
+        bytes_sb = [sbuf("bytes_sb%d" % s, [P, ROW_TILES, D], U8) for s in range(S)]
+        scale_sb = sbuf("scale_sb", [P, PACK], F32)
+        bias_bf = sbuf("bias_bf", [P, 1], BF16)
+        bias_sb = sbuf("bias_sb", [P, 1], F32)
+        ident = sbuf("ident", [P, P], F32)
+        zeros = sbuf("zeros", [P, BANK], BF16)
+        table_in = sbuf("table_in", [P, 1], F32)
+        table_out = sbuf("table_out", [P, 1], F32)
 
-        a_in = tensor0.rearrange("s (g p r) e -> s p g r e", p=P, r=2)
-        b_in = tensor1_bytes.rearrange("s (p r) d -> s p r d", r=8)
-        pair_view = out.rearrange("b s (p h r) j -> s h p b (r j)", h=4, r=2)
-        out_view = out.rearrange("b s (p r) j -> s r p b j", r=8)
+        kernel_codes = sbuf("kernel_codes", [P, D], U32)
+        kernel_scales = sbuf("kernel_scales", [P, D], U8)
+        q_codes = [sbuf("q_codes%d" % s, [P, N], U32) for s in range(S)]
+        q_scales = [sbuf("q_scales%d" % s, [P, N], U8) for s in range(S)]
+        out_sb = {(s, x): sbuf("out_sb%d%d" % (s, x), [P, 2, N], F32) for s in range(S) for x in range(ROW_TILES // 2)}
+        banks, packed, wide, codes, scales = {}, {}, {}, {}, {}
 
-        with tc.manual_schedule():
-            k_in = kernel.rearrange("(p t) e -> p t e", t=4)
-            nc.sync.dma_start(out=k_sb[:, 0:2, :], in_=k_in[:, 0:2, :])
-            nc.sync.dma_start(out=k_sb[:, 2:4, :], in_=k_in[:, 2:4, :])
-            nc.sync.dma_start(out=a_sb[0][:, 0], in_=a_in[0][:, 0])
-            nc.sync.dma_start(out=b_sb[0][:, 0:2, :], in_=b_in[0][:, 0:2, :])
-            nc.sync.dma_start(out=scale_sb[:], in_=tensor1_scale.rearrange("a b (p t) -> p (a b t)", t=4))
-            nc.sync.dma_start(out=a_sb[0][:, 1], in_=a_in[0][:, 1])
-            nc.sync.dma_start(out=bias_bf[:], in_=bias.partition_broadcast(P))
-            nc.sync.dma_start(out=b_sb[0][:, 2:8, :], in_=b_in[0][:, 2:8, :])
-            nc.sync.dma_start(out=a_sb[0][:, 2:4], in_=a_in[0][:, 2:4])
-            nc.sync.dma_start(out=a_sb[1][:], in_=a_in[1])
-            nc.sync.dma_start(out=b_sb[1][:], in_=b_in[1])
-            nc.vector.memset(dummy[:], 0.0)
-            make_identity(nc, ident[:])
-            nc.gpsimd.memset(warm[:], 0.0)
-            nc.gpsimd.tensor_copy(out=bias_sb[:], in_=bias_bf[:])
-            nc.scalar.activation(out=warm_out[:], in_=warm[:], func=ACT.Identity)
 
-            def copy(eng, out, in_):
-                if eng == "S":
-                    nc.scalar.copy(out, in_)
-                else:
-                    nc.vector.tensor_copy(out=out, in_=in_)
+        def copy(engine, dst, src):
+            if engine == "scalar":
+                nc.scalar.copy(dst, src)
+            else:
+                nc.vector.tensor_copy(out=dst, in_=src)
 
-            def spin(n):
-                t = bank()
-                for x in range(n):
-                    nc.tensor.matmul(t[:], lhsT=dummy[:, 0:P], rhs=dummy[:], start=True, stop=True)
+        def spin(count):
+            t = psum_bank()
+            for i in range(count):
+                nc.tensor.matmul(t[:], lhsT=zeros[:, 0:P], rhs=zeros[:], start=True, stop=True)
 
-            def transpose_rows(key, rows):
-                t = bank()
-                banks[key] = t
-                for r, row in enumerate(rows):
-                    words = row.bitcast(F32)
-                    for u in (0, 1):
-                        c = (len(rows) * u + r) * P
-                        nc.tensor.transpose(t[:, c : c + P], words[:, u::2], ident[:])
+        def transpose(key, rows):
+            t = psum_bank()
+            banks[key] = t
+            for x, piece in enumerate(rows):
+                words = piece.bitcast(F32)
+                for u in (0, 1):
+                    c = (len(rows) * u + x) * P
+                    nc.tensor.transpose(t[:, c : c + P], words[:, u::2], ident[:])
 
-            def cast_b(s, r, eng):
-                w = sb("wide%d%d" % (s, r), [P, 2 * D], BF16)
-                wide[s, r] = w[:, 0:D]
-                wide[s, r + 1] = w[:, D : 2 * D]
-                copy(eng, w[:], b_sb[s][:, r : r + 2, :].rearrange("p r d -> p (r d)").bitcast(FP8))
+        def quantize(code_words, scale_bytes, values):
+            nc.vector.quantize_mx(out=code_words.bitcast(FP8X4), scales=scale_bytes, in_=values)
 
-            def t_b(s, r, n):
-                transpose_rows(("B", s, r), [wide[s, r + x] for x in range(n)])
+        def kernel_transpose(half):
+            transpose(("k", half), [kernel_sb[:, 2 * half + x, :] for x in (0, 1)])
 
-            def prod_b(s, r, n):
-                g = sb("gb%d%d" % (s, r), [P, n * 512], BF16)
-                grouped["B", s, r] = g
-                nc.vector.tensor_tensor(
-                    out=g[:].rearrange("p (c u e) -> p c u e", u=2, e=2),
-                    in0=banks["B", s, r][:, 0 : n * 256].bitcast(BF16).rearrange("p (u c e) -> p c u e", u=2, e=2),
-                    in1=scale_sb[:].unsqueeze(1).to_broadcast([P, n * P, 4]).rearrange("p c (u e) -> p c u e", u=2),
-                    op=ALU.mult,
-                )
+        def kernel_copy(half, engine):
+            dst = sbuf("kernel_packed%d" % half, [P, GROUP * PACK], BF16)
+            packed["k", half] = dst
+            copy(
+                engine,
+                dst[:].bitcast(F32).rearrange("p (c u) -> p c u", u=2),
+                banks["k", half][:].rearrange("p (u c) -> p c u", u=2),
+            )
 
-            def quant(codes, scales, g):
-                nc.vector.quantize_mx(out=codes.bitcast(FP8X4), scales=scales, in_=g)
+        def kernel_quantize(half):
+            cols = slice(half * GROUP, (half + 1) * GROUP)
+            quantize(kernel_codes[:, cols], kernel_scales[:, cols], packed["k", half][:])
 
-            def q_b(s, r, n):
-                c = sb("bc%d%d" % (s, r), [P, n * P], U32)
-                z = sb("bs%d%d" % (s, r), [P, n * P], U8)
-                quant(c[:], z[:], grouped["B", s, r][:])
-                for x in range(n):
-                    b_codes[s, r + x] = c[:, x * P : (x + 1) * P]
-                    b_scales[s, r + x] = z[:, x * P : (x + 1) * P]
+        def t0_transpose(s, g):
+            transpose(("t0", s, g), [tensor0_sb[s][:, g, h, :] for h in (0, 1)])
 
-            def t_k(h):
-                transpose_rows(("K", h), [k_sb[:, 2 * h, :], k_sb[:, 2 * h + 1, :]])
+        def t0_copy(s, g, engine):
+            dst = sbuf("t0_packed%d%d" % (s, g), [P, GROUP * PACK], BF16)
+            packed["t0", s, g] = dst
+            copy(
+                engine,
+                dst[:].bitcast(F32).rearrange("p (m h u) -> p m h u", h=2, u=2),
+                banks["t0", s, g][:].rearrange("p (u h m) -> p m h u", u=2, h=2),
+            )
 
-            def cp_k(h, eng):
-                g = sb("gk%d" % h, [P, 1024], BF16)
-                grouped["K", h] = g
-                copy(
-                    eng,
-                    g[:].bitcast(F32).rearrange("p (c u) -> p c u", u=2),
-                    banks["K", h][:].rearrange("p (u c) -> p c u", u=2),
-                )
+        def t0_quantize(s, g):
+            codes["t0", s, g] = sbuf("t0_codes%d%d" % (s, g), [P, GROUP], U32)
+            scales["t0", s, g] = sbuf("t0_scales%d%d" % (s, g), [P, GROUP], U8)
+            quantize(codes["t0", s, g][:], scales["t0", s, g][:], packed["t0", s, g][:])
 
-            def q_k(h):
-                quant(k_codes[:, 256 * h : 256 * h + 256], k_scales[:, 256 * h : 256 * h + 256], grouped["K", h][:])
-
-            def t_a(s, g):
-                transpose_rows(("A", s, g), [a_sb[s][:, g, 0, :], a_sb[s][:, g, 1, :]])
-
-            def cp_a(s, g, eng):
-                t = sb("ga%d%d" % (s, g), [P, 1024], BF16)
-                grouped["A", s, g] = t
-                copy(
-                    eng,
-                    t[:].bitcast(F32).rearrange("p (m r u) -> p m r u", r=2, u=2),
-                    banks["A", s, g][:].rearrange("p (u r m) -> p m r u", u=2, r=2),
-                )
-
-            def q_a(s, g):
-                a_codes[s, g] = sb("ac%d%d" % (s, g), [P, 256], U32)
-                a_scales[s, g] = sb("as%d%d" % (s, g), [P, 256], U8)
-                quant(a_codes[s, g][:], a_scales[s, g][:], grouped["A", s, g][:])
-
-            def m1(s, g, h):
-                t = bank()
-                banks["Q", s, g, h] = t
-                cols = slice(h * P, (h + 1) * P)
-                for c in range(4):
-                    rows = slice(c * P, (c + 1) * P)
-                    nc.tensor.matmul_mx(
-                        out=t[:, rows],
-                        lhsT=k_codes[:, rows].bitcast(FP8X4),
-                        lhsT_scale=k_scales[:, rows],
-                        rhs=a_codes[s, g][:, cols].bitcast(FP8X4),
-                        rhs_scale=a_scales[s, g][:, cols],
-                        start=True,
-                        stop=True,
-                    )
-
-            def cp_q(s, g, h, eng):
-                if ("Q", s, g) not in grouped:
-                    grouped["Q", s, g] = sb("gq%d%d" % (s, g), [P, 1024], BF16)
-                copy(
-                    eng,
-                    grouped["Q", s, g][:, h * 512 : h * 512 + 512].rearrange("p (j t) -> p j t", t=4),
-                    banks["Q", s, g, h][:].rearrange("p (t j) -> p j t", t=4),
-                )
-
-            def q_q(s, g):
-                cols = slice(g * 256, g * 256 + 256)
-                quant(q_codes[s][:, cols], q_scales[s][:, cols], grouped["Q", s, g][:])
-
-            def m2(s, r, lo, hi):
-                t = bank()
-                banks["O", s, r, lo] = t
+        def q_matmul(s, g, half):
+            t = psum_bank()
+            banks["q", s, g, half] = t
+            js = slice(half * P, (half + 1) * P)
+            for x in range(PACK):
+                ms = slice(x * P, (x + 1) * P)
                 nc.tensor.matmul_mx(
-                    out=t[:, 0 : hi - lo],
-                    lhsT=b_codes[s, r].bitcast(FP8X4),
-                    lhsT_scale=b_scales[s, r],
-                    rhs=q_codes[s][:, lo:hi].bitcast(FP8X4),
-                    rhs_scale=q_scales[s][:, lo:hi],
+                    out=t[:, ms],
+                    lhsT=kernel_codes[:, ms].bitcast(FP8X4),
+                    lhsT_scale=kernel_scales[:, ms],
+                    rhs=codes["t0", s, g][:, js].bitcast(FP8X4),
+                    rhs_scale=scales["t0", s, g][:, js],
                     start=True,
                     stop=True,
                 )
 
-            def ev(s, r, lo, hi, eng):
-                if (s, r // 2) not in outs:
-                    outs[s, r // 2] = sb("o%d%d" % (s, r), [P, 2, N], F32)
-                o = outs[s, r // 2][:, r % 2, lo:hi]
-                t = banks["O", s, r, lo][:, 0 : hi - lo]
-                if eng == "S":
-                    nc.scalar.activation(out=o, in_=t, func=ACT.Identity, bias=bias_sb[:])
+        def q_copy(s, g, half, engine):
+            if half == 0:
+                packed["q", s, g] = sbuf("q_packed%d%d" % (s, g), [P, GROUP * PACK], BF16)
+            dst = packed["q", s, g][:, half * BANK : (half + 1) * BANK]
+            copy(engine, dst.rearrange("p (j t) -> p j t", t=PACK), banks["q", s, g, half][:].rearrange("p (t j) -> p j t", t=PACK))
+
+        def q_quantize(s, g):
+            cols = slice(g * GROUP, (g + 1) * GROUP)
+            quantize(q_codes[s][:, cols], q_scales[s][:, cols], packed["q", s, g][:])
+
+        def t1_widen(s, r):
+            dst = sbuf("t1_wide%d%d" % (s, r), [P, 2 * D], BF16)
+            wide[s, r], wide[s, r + 1] = dst[:, 0:D], dst[:, D : 2 * D]
+            nc.vector.tensor_copy(out=dst[:], in_=bytes_sb[s][:, r : r + 2, :].rearrange("p r d -> p (r d)").bitcast(FP8))
+
+        def t1_transpose(s, r, count):
+            transpose(("t1", s, r), [wide[s, r + x] for x in range(count)])
+
+        def t1_scale(s, r, count):
+            dst = sbuf("t1_packed%d%d" % (s, r), [P, count * P * PACK], BF16)
+            packed["t1", s, r] = dst
+            bank = banks["t1", s, r][:, 0 : count * P * 2].bitcast(BF16)
+            every_column = scale_sb[:].unsqueeze(1).to_broadcast([P, count * P, PACK])
+            nc.vector.tensor_tensor(
+                out=dst[:].rearrange("p (c u e) -> p c u e", u=2, e=2),
+                in0=bank.rearrange("p (u c e) -> p c u e", u=2, e=2),
+                in1=every_column.rearrange("p c (u e) -> p c u e", u=2),
+                op=MULT,
+            )
+
+        def t1_quantize(s, r, count):
+            words = sbuf("t1_codes%d%d" % (s, r), [P, count * P], U32)
+            planes = sbuf("t1_scales%d%d" % (s, r), [P, count * P], U8)
+            quantize(words[:], planes[:], packed["t1", s, r][:])
+            for x in range(count):
+                cols = slice(x * P, (x + 1) * P)
+                codes["t1", s, r + x], scales["t1", s, r + x] = words[:, cols], planes[:, cols]
+
+        def score_matmul(s, r, lo, hi):
+            t = psum_bank()
+            banks["score", s, r, lo] = t
+            nc.tensor.matmul_mx(
+                out=t[:, 0 : hi - lo],
+                lhsT=codes["t1", s, r].bitcast(FP8X4),
+                lhsT_scale=scales["t1", s, r],
+                rhs=q_codes[s][:, lo:hi].bitcast(FP8X4),
+                rhs_scale=q_scales[s][:, lo:hi],
+                start=True,
+                stop=True,
+            )
+
+        def score_copy(s, r, lo, hi, engine):
+            src = banks["score", s, r, lo][:, 0 : hi - lo]
+            dst = out_sb[s, r // 2][:, r % 2, lo:hi]
+            if engine == "scalar":
+                nc.scalar.activation(out=dst, in_=src, func=IDENTITY, bias=bias_sb[:])
+            else:
+                nc.vector.tensor_scalar(out=dst, in0=src, scalar1=bias_sb[:], scalar2=None, op0=ADD)
+
+        out_rows = out.rearrange("b s (p r) j -> s r p b j", r=ROW_TILES)
+        out_pairs = out.rearrange("b s (p x r) j -> s x p b (r j)", x=ROW_TILES // 2, r=2)
+
+        def store(s, r, lo, hi):
+            src = out_sb[s, r // 2][:, r % 2, lo:hi]
+            nc.sync.dma_start(out=out_rows[s, r][:, :, lo:hi], in_=src.unsqueeze(1).to_broadcast([P, COPIES, hi - lo]))
+
+        def store_pair(s, x):
+            src = out_sb[s, x][:].rearrange("p r j -> p (r j)")
+            nc.sync.dma_start(out=out_pairs[s, x], in_=src.unsqueeze(1).to_broadcast([P, COPIES, 2 * N]))
+
+        def score_rows(s, tiles, engines, after_row):
+            for x in range(len(tiles) + 1):
+                if x < len(tiles):
+                    for lo in (0, HALF):
+                        score_matmul(s, tiles[x], lo, lo + HALF)
+                if x > 0:
+                    for lo, engine in zip((0, HALF), engines):
+                        score_copy(s, tiles[x - 1], lo, lo + HALF, engine)
+                    after_row(tiles[x - 1])
+
+        kernel_in = kernel.rearrange("(m t) e -> m t e", t=PACK)
+        tensor0_in = tensor0.rearrange("s (g p h) e -> s p g h e", p=P, h=2)
+        bytes_in = tensor1_bytes.rearrange("s (p r) d -> s p r d", r=ROW_TILES)
+        nc.sync.dma_start(out=bytes_sb[0][:, 0:2, :], in_=bytes_in[0][:, 0:2, :])
+        for half in (0, 1):
+            ts = slice(2 * half, 2 * half + 2)
+            nc.sync.dma_start(out=kernel_sb[:, ts, :], in_=kernel_in[:, ts, :])
+        nc.sync.dma_start(out=scale_sb[:], in_=tensor1_scale.rearrange("a b (p t) -> p (a b t)", t=PACK))
+        for g in range(N // GROUP):
+            nc.sync.dma_start(out=tensor0_sb[0][:, g], in_=tensor0_in[0][:, g])
+        nc.sync.dma_start(out=bias_bf[:], in_=bias.partition_broadcast(P))
+        nc.sync.dma_start(out=bytes_sb[0][:, 2:ROW_TILES, :], in_=bytes_in[0][:, 2:ROW_TILES, :])
+        nc.sync.dma_start(out=tensor0_sb[1][:], in_=tensor0_in[1])
+        nc.sync.dma_start(out=bytes_sb[1][:], in_=bytes_in[1])
+
+        nc.vector.memset(zeros[:], 0.0)
+        make_identity(nc, ident[:])
+        nc.gpsimd.memset(table_in[:], 0.0)
+        nc.scalar.activation(out=table_out[:], in_=table_in[:], func=IDENTITY)
+        nc.gpsimd.tensor_copy(out=bias_sb[:], in_=bias_bf[:])
+
+        spin(4)
+        t1_widen(0, 0)
+        kernel_transpose(0)
+        spin(1)
+        t1_transpose(0, 0, 1)
+        t1_scale(0, 0, 1)
+        kernel_copy(0, "scalar")
+        kernel_transpose(1)
+        spin(1)
+        kernel_quantize(0)
+        t0_transpose(0, 0)
+        t1_transpose(0, 1, 1)
+        kernel_copy(1, "scalar")
+        spin(1)
+        t0_transpose(0, 1)
+        t1_scale(0, 1, 1)
+        t0_copy(0, 0, "scalar")
+        kernel_quantize(1)
+        t0_transpose(0, 2)
+        spin(1)
+        t0_transpose(0, 3)
+        t0_copy(0, 1, "scalar")
+        t0_quantize(0, 0)
+        t1_quantize(0, 0, 1)
+        q_matmul(0, 0, 0)
+        t0_quantize(0, 1)
+        t1_widen(0, 2)
+        t0_copy(0, 2, "scalar")
+        q_matmul(0, 0, 1)
+        q_matmul(0, 1, 0)
+        t1_quantize(0, 1, 1)
+        t0_copy(0, 3, "scalar")
+        q_copy(0, 0, 0, "scalar")
+        q_matmul(0, 1, 1)
+        t1_transpose(0, 2, 2)
+        t0_quantize(0, 2)
+        t0_quantize(0, 3)
+        q_matmul(0, 2, 0)
+        q_copy(0, 0, 1, "scalar")
+        q_copy(0, 1, 0, "scalar")
+        q_copy(0, 1, 1, "scalar")
+        t1_widen(0, 4)
+        q_quantize(0, 0)
+        t1_scale(0, 2, 2)
+        q_matmul(0, 2, 1)
+        q_matmul(0, 3, 0)
+        q_copy(0, 2, 0, "scalar")
+        q_quantize(0, 1)
+        score_matmul(0, 0, 0, GROUP)
+        score_matmul(0, 1, 0, GROUP)
+        q_matmul(0, 3, 1)
+        t1_transpose(0, 4, 2)
+        score_copy(0, 0, 0, GROUP, "scalar")
+        store(0, 0, 0, GROUP)
+        score_copy(0, 1, 0, GROUP, "vector")
+        store(0, 1, 0, GROUP)
+        t1_quantize(0, 2, 2)
+        score_matmul(0, 0, GROUP, HALF)
+        score_matmul(0, 1, GROUP, HALF)
+        q_copy(0, 2, 1, "scalar")
+        q_copy(0, 3, 0, "vector")
+        q_copy(0, 3, 1, "scalar")
+        q_quantize(0, 2)
+        score_copy(0, 0, GROUP, HALF, "scalar")
+        store(0, 0, GROUP, HALF)
+        q_quantize(0, 3)
+        t1_scale(0, 4, 2)
+        score_copy(0, 1, GROUP, HALF, "scalar")
+        store(0, 1, GROUP, HALF)
+        score_matmul(0, 2, 0, HALF)
+        score_matmul(0, 3, 0, HALF)
+        for r in (2, 3):
+            score_copy(0, r, 0, HALF, "scalar")
+            store(0, r, 0, HALF)
+        for r in range(4):
+            score_matmul(0, r, HALF, N)
+        t1_widen(0, 6)
+        t1_quantize(0, 4, 2)
+        for r in range(4):
+            score_copy(0, r, HALF, N, "vector" if r == 1 else "scalar")
+            store(0, r, HALF, N)
+
+        def store_row(r):
+            store(0, r, 0, N)
+
+        def store_second_of_pair(s):
+            def after_row(r):
+                if r % 2 == 1:
+                    store_pair(s, r // 2)
+
+            return after_row
+
+        score_rows(0, [4, 5], ("scalar", "scalar"), store_row)
+        for r in range(0, ROW_TILES, 2):
+            t1_widen(1, r)
+
+        units = [("t1", 0, 6)] + [("t0", 1, g) for g in range(N // GROUP)] + [("t1", 1, r) for r in range(0, ROW_TILES, 2)]
+        for x in range(len(units) + 2):
+            if x < len(units):
+                kind, s, y = units[x]
+                if kind == "t0":
+                    t0_transpose(s, y)
                 else:
-                    nc.vector.tensor_scalar(out=o, in0=t, scalar1=bias_sb[:], scalar2=None, op0=ALU.add)
+                    t1_transpose(s, y, 2)
+            if 1 <= x <= len(units):
+                kind, s, y = units[x - 1]
+                if kind == "t0":
+                    t0_copy(s, y, "scalar")
+                else:
+                    t1_scale(s, y, 2)
+            if x >= 2:
+                kind, s, y = units[x - 2]
+                if kind == "t0":
+                    t0_quantize(s, y)
+                else:
+                    t1_quantize(s, y, 2)
+            if x == len(units) - 3:
+                score_rows(0, [6, 7], ("scalar", "scalar"), store_second_of_pair(0))
 
-            def store(s, r, lo, hi):
-                nc.sync.dma_start(
-                    out=out_view[s, r][:, :, lo:hi],
-                    in_=outs[s, r // 2][:, r % 2, lo:hi].unsqueeze(1).to_broadcast([P, 2, hi - lo]),
-                )
+        for g in range(N // GROUP + 2):
+            if g < N // GROUP:
+                for half in (0, 1):
+                    q_matmul(1, g, half)
+            if 1 <= g <= N // GROUP:
+                for half in (0, 1):
+                    q_copy(1, g - 1, half, "scalar")
+            if g >= 2:
+                q_quantize(1, g - 2)
 
-            def store_pair(s, r):
-                nc.sync.dma_start(
-                    out=pair_view[s, r // 2],
-                    in_=outs[s, r // 2][:].rearrange("p r j -> p (r j)").unsqueeze(1).to_broadcast([P, 2, 2 * N]),
-                )
+        def store_last(r):
+            if r < 2:
+                store(1, r, 0, N)
+            elif r % 2 == 1:
+                store_pair(1, r // 2)
 
-            steps = [
-                (spin, 5),
-                (t_k, 0),
-                (cp_k, 0, "V"),
-                (q_k, 0),
-                (t_k, 1),
-                (spin, 1),
-                (cast_b, 0, 0, "V"),
-                (t_a, 0, 0),
-                (spin, 1),
-                (cp_k, 1, "S"),
-                (q_k, 1),
-                (cp_a, 0, 0, "S"),
-                (q_a, 0, 0),
-                (cast_b, 0, 6, "V"),
-                (t_a, 0, 1),
-                (cp_a, 0, 1, "S"),
-                (t_b, 0, 0, 1),
-                (cast_b, 0, 2, "S"),
-                (prod_b, 0, 0, 1),
-                (q_a, 0, 1),
-                (t_b, 0, 1, 1),
-                (spin, 1),
-                (prod_b, 0, 1, 1),
-                (q_b, 0, 1, 1),
-                (m1, 0, 0, 1),
-                (m1, 0, 0, 0),
-                (t_a, 0, 2),
-                (cp_q, 0, 0, 1, "S"),
-                (q_b, 0, 0, 1),
-                (t_b, 0, 2, 2),
-                (prod_b, 0, 2, 2),
-                (cp_q, 0, 0, 0, "S"),
-                (t_a, 0, 3),
-                (cp_a, 0, 2, "S"),
-                (cp_a, 0, 3, "S"),
-                (m1, 0, 1, 0),
-                (cp_q, 0, 1, 0, "S"),
-                (q_q, 0, 0),
-                (m1, 0, 1, 1),
-                (cp_q, 0, 1, 1, "S"),
-                (m2, 0, 0, 0, 256),
-                (q_a, 0, 3),
-                (m1, 0, 3, 1),
-                (ev, 0, 0, 0, 256, "S"),
-                (store, 0, 0, 0, 256),
-                (m2, 0, 1, 0, 256),
-                (ev, 0, 1, 0, 256, "S"),
-                (store, 0, 1, 0, 256),
-                (q_a, 0, 2),
-                (m1, 0, 2, 0),
-                (cp_q, 0, 2, 0, "S"),
-                (q_b, 0, 2, 2),
-                (q_q, 0, 1),
-                (m1, 0, 3, 0),
-                (m2, 0, 1, 256, 512),
-                (ev, 0, 1, 256, 512, "S"),
-                (store, 0, 1, 256, 512),
-                (m2, 0, 0, 256, 512),
-                (ev, 0, 0, 256, 512, "S"),
-                (store, 0, 0, 256, 512),
-                (m1, 0, 2, 1),
-                (m2, 0, 3, 0, 512),
-                (m2, 0, 2, 0, 512),
-                (ev, 0, 2, 0, 512, "S"),
-                (store, 0, 2, 0, 512),
-                (ev, 0, 3, 0, 512, "S"),
-                (store, 0, 3, 0, 512),
-                (cp_q, 0, 3, 1, "V"),
-                (t_a, 1, 1),
-                (cp_a, 1, 1, "S"),
-                (cast_b, 0, 4, "V"),
-                (cp_q, 0, 3, 0, "V"),
-                (cp_q, 0, 2, 1, "V"),
-                (t_b, 0, 4, 2),
-                (t_a, 1, 2),
-                (t_a, 1, 3),
-                (q_q, 0, 3),
-                (q_q, 0, 2),
-                (prod_b, 0, 4, 2),
-                (q_b, 0, 4, 2),
-                (m2, 0, 0, 512, 1024),
-                (ev, 0, 0, 512, 1024, "V"),
-                (store, 0, 0, 512, 1024),
-                (cp_a, 1, 3, "S"),
-                (cast_b, 1, 6, "S"),
-                (cast_b, 1, 0, "S"),
-                (q_a, 1, 3),
-                (m2, 0, 1, 512, 1024),
-                (ev, 0, 1, 512, 1024, "V"),
-                (store, 0, 1, 512, 1024),
-                (m2, 0, 2, 512, 1024),
-                (t_a, 1, 0),
-                (cp_a, 1, 0, "V"),
-                (m2, 0, 3, 512, 1024),
-                (m1, 1, 3, 1),
-                (ev, 0, 3, 512, 1024, "S"),
-                (store, 0, 3, 512, 1024),
-                (m2, 0, 5, 0, 512),
-                (q_a, 1, 0),
-                (ev, 0, 2, 512, 1024, "V"),
-                (store, 0, 2, 512, 1024),
-                (q_a, 1, 1),
-                (m2, 0, 4, 512, 1024),
-                (m2, 0, 5, 512, 1024),
-                (t_b, 0, 6, 2),
-                (prod_b, 0, 6, 2),
-                (q_b, 0, 6, 2),
-                (cp_q, 1, 3, 1, "S"),
-                (ev, 0, 5, 512, 1024, "S"),
-                (cp_a, 1, 2, "S"),
-                (t_b, 1, 6, 2),
-                (q_a, 1, 2),
-                (m1, 1, 1, 1),
-                (m1, 1, 0, 1),
-                (m1, 1, 3, 0),
-                (cast_b, 1, 2, "V"),
-                (m1, 1, 0, 0),
-                (ev, 0, 5, 0, 512, "S"),
-                (store, 0, 5, 0, 1024),
-                (cast_b, 1, 4, "V"),
-                (cp_q, 1, 0, 1, "S"),
-                (cp_q, 1, 1, 1, "S"),
-                (m1, 1, 1, 0),
-                (m1, 1, 2, 0),
-                (cp_q, 1, 1, 0, "S"),
-                (cp_q, 1, 3, 0, "S"),
-                (m2, 0, 4, 0, 512),
-                (ev, 0, 4, 0, 512, "V"),
-                (t_b, 1, 2, 2),
-                (m2, 0, 7, 512, 1024),
-                (prod_b, 1, 2, 2),
-                (ev, 0, 4, 512, 1024, "S"),
-                (store, 0, 4, 0, 1024),
-                (cp_q, 1, 2, 0, "S"),
-                (q_b, 1, 2, 2),
-                (m2, 0, 6, 512, 1024),
-                (ev, 0, 6, 512, 1024, "V"),
-                (m2, 0, 6, 0, 512),
-                (ev, 0, 7, 512, 1024, "S"),
-                (t_b, 1, 4, 2),
-                (ev, 0, 6, 0, 512, "V"),
-                (q_q, 1, 3),
-                (q_q, 1, 1),
-                (m2, 0, 7, 0, 512),
-                (ev, 0, 7, 0, 512, "S"),
-                (store_pair, 0, 6),
-                (m1, 1, 2, 1),
-                (cp_q, 1, 0, 0, "S"),
-                (q_q, 1, 0),
-                (cp_q, 1, 2, 1, "S"),
-                (t_b, 1, 0, 2),
-                (prod_b, 1, 0, 2),
-                (q_q, 1, 2),
-                (m2, 1, 2, 0, 512),
-                (ev, 1, 2, 0, 512, "S"),
-                (q_b, 1, 0, 2),
-                (m2, 1, 3, 0, 512),
-                (ev, 1, 3, 0, 512, "S"),
-                (m2, 1, 3, 512, 1024),
-                (m2, 1, 2, 512, 1024),
-                (ev, 1, 2, 512, 1024, "V"),
-                (prod_b, 1, 6, 2),
-                (q_b, 1, 6, 2),
-                (ev, 1, 3, 512, 1024, "S"),
-                (store_pair, 1, 2),
-                (m2, 1, 1, 512, 1024),
-                (m2, 1, 0, 0, 512),
-                (prod_b, 1, 4, 2),
-                (m2, 1, 7, 0, 512),
-                (ev, 1, 7, 0, 512, "S"),
-                (q_b, 1, 4, 2),
-                (m2, 1, 7, 512, 1024),
-                (ev, 1, 7, 512, 1024, "S"),
-                (m2, 1, 6, 0, 512),
-                (ev, 1, 6, 0, 512, "V"),
-                (m2, 1, 0, 512, 1024),
-                (m2, 1, 6, 512, 1024),
-                (ev, 1, 6, 512, 1024, "S"),
-                (store_pair, 1, 6),
-                (ev, 1, 0, 512, 1024, "S"),
-                (m2, 1, 5, 0, 512),
-                (ev, 1, 1, 512, 1024, "V"),
-                (ev, 1, 5, 0, 512, "S"),
-                (m2, 1, 1, 0, 512),
-                (m2, 1, 4, 512, 1024),
-                (ev, 1, 4, 512, 1024, "S"),
-                (ev, 1, 1, 0, 512, "S"),
-                (m2, 1, 4, 0, 512),
-                (ev, 1, 4, 0, 512, "V"),
-                (m2, 1, 5, 512, 1024),
-                (ev, 1, 5, 512, 1024, "V"),
-                (store_pair, 1, 4),
-                (ev, 1, 0, 0, 512, "S"),
-                (store_pair, 1, 0),
-            ]
-            for step in steps:
-                step[0](*step[1:])
+        score_rows(1, list(range(ROW_TILES)), ("scalar", "vector"), store_last)

from contextlib import ExitStack

import concourse.mybir as mybir
from concourse.masks import make_identity

F32 = mybir.dt.float32
BF16 = mybir.dt.bfloat16
U32 = mybir.dt.uint32
U8 = mybir.dt.uint8
FP8 = mybir.dt.float8_e4m3fn
FP8X4 = mybir.dt.float8_e4m3fn_x4
IDENTITY = mybir.ActivationFunctionType.Identity
ADD = mybir.AluOpType.add
MULT = mybir.AluOpType.mult

P = 128
COPIES, S, N, D = 2, 2, 1024, 512
PACK = 4
BANK = 512
GROUP = 256
ROW_TILES = N // P
HALF = N // 2

FLOPS = 2 * S * N * D * D + 2 * S * N * N * D


def tile_bilinear_kernel(tc, tensor0, tensor1_bytes, tensor1_scale, kernel, bias, out):
    nc = tc.nc

    with ExitStack() as ctx:
        keep = ctx.enter_context(tc.tile_pool(name="keep", bufs=1))
        psum = ctx.enter_context(tc.psum_pool(name="psum", bufs=8))
        ctx.enter_context(tc.manual_schedule())

        def sbuf(name, shape, dtype):
            return keep.tile(shape, dtype, name=name, align_bytes=64)

        def psum_bank():
            return psum.tile([P, BANK], F32, name="bank")

        kernel_sb = sbuf("kernel_sb", [P, PACK, D], BF16)
        tensor0_sb = [sbuf("tensor0_sb%d" % s, [P, N // GROUP, 2, D], BF16) for s in range(S)]
        bytes_sb = [sbuf("bytes_sb%d" % s, [P, ROW_TILES, D], U8) for s in range(S)]
        scale_sb = sbuf("scale_sb", [P, PACK], F32)
        bias_bf = sbuf("bias_bf", [P, 1], BF16)
        bias_sb = sbuf("bias_sb", [P, 1], F32)
        ident = sbuf("ident", [P, P], F32)
        zeros = sbuf("zeros", [P, BANK], BF16)
        table_in = sbuf("table_in", [P, 1], F32)
        table_out = sbuf("table_out", [P, 1], F32)

        kernel_codes = sbuf("kernel_codes", [P, D], U32)
        kernel_scales = sbuf("kernel_scales", [P, D], U8)
        q_codes = [sbuf("q_codes%d" % s, [P, N], U32) for s in range(S)]
        q_scales = [sbuf("q_scales%d" % s, [P, N], U8) for s in range(S)]
        out_sb = {(s, x): sbuf("out_sb%d%d" % (s, x), [P, 2, N], F32) for s in range(S) for x in range(ROW_TILES // 2)}
        banks, packed, wide, codes, scales = {}, {}, {}, {}, {}


        def copy(engine, dst, src):
            if engine == "scalar":
                nc.scalar.copy(dst, src)
            else:
                nc.vector.tensor_copy(out=dst, in_=src)

        def spin(count):
            t = psum_bank()
            for i in range(count):
                nc.tensor.matmul(t[:], lhsT=zeros[:, 0:P], rhs=zeros[:], start=True, stop=True)

        def transpose(key, rows):
            t = psum_bank()
            banks[key] = t
            for x, piece in enumerate(rows):
                words = piece.bitcast(F32)
                for u in (0, 1):
                    c = (len(rows) * u + x) * P
                    nc.tensor.transpose(t[:, c : c + P], words[:, u::2], ident[:])

        def quantize(code_words, scale_bytes, values):
            nc.vector.quantize_mx(out=code_words.bitcast(FP8X4), scales=scale_bytes, in_=values)

        def kernel_transpose(half):
            transpose(("k", half), [kernel_sb[:, 2 * half + x, :] for x in (0, 1)])

        def kernel_copy(half, engine):
            dst = sbuf("kernel_packed%d" % half, [P, GROUP * PACK], BF16)
            packed["k", half] = dst
            copy(
                engine,
                dst[:].bitcast(F32).rearrange("p (c u) -> p c u", u=2),
                banks["k", half][:].rearrange("p (u c) -> p c u", u=2),
            )

        def kernel_quantize(half):
            cols = slice(half * GROUP, (half + 1) * GROUP)
            quantize(kernel_codes[:, cols], kernel_scales[:, cols], packed["k", half][:])

        def t0_transpose(s, g):
            transpose(("t0", s, g), [tensor0_sb[s][:, g, h, :] for h in (0, 1)])

        def t0_copy(s, g, engine):
            dst = sbuf("t0_packed%d%d" % (s, g), [P, GROUP * PACK], BF16)
            packed["t0", s, g] = dst
            copy(
                engine,
                dst[:].bitcast(F32).rearrange("p (m h u) -> p m h u", h=2, u=2),
                banks["t0", s, g][:].rearrange("p (u h m) -> p m h u", u=2, h=2),
            )

        def t0_quantize(s, g):
            codes["t0", s, g] = sbuf("t0_codes%d%d" % (s, g), [P, GROUP], U32)
            scales["t0", s, g] = sbuf("t0_scales%d%d" % (s, g), [P, GROUP], U8)
            quantize(codes["t0", s, g][:], scales["t0", s, g][:], packed["t0", s, g][:])

        def q_matmul(s, g, half):
            t = psum_bank()
            banks["q", s, g, half] = t
            js = slice(half * P, (half + 1) * P)
            for x in range(PACK):
                ms = slice(x * P, (x + 1) * P)
                nc.tensor.matmul_mx(
                    out=t[:, ms],
                    lhsT=kernel_codes[:, ms].bitcast(FP8X4),
                    lhsT_scale=kernel_scales[:, ms],
                    rhs=codes["t0", s, g][:, js].bitcast(FP8X4),
                    rhs_scale=scales["t0", s, g][:, js],
                    start=True,
                    stop=True,
                )

        def q_copy(s, g, half, engine):
            if half == 0:
                packed["q", s, g] = sbuf("q_packed%d%d" % (s, g), [P, GROUP * PACK], BF16)
            dst = packed["q", s, g][:, half * BANK : (half + 1) * BANK]
            copy(engine, dst.rearrange("p (j t) -> p j t", t=PACK), banks["q", s, g, half][:].rearrange("p (t j) -> p j t", t=PACK))

        def q_quantize(s, g):
            cols = slice(g * GROUP, (g + 1) * GROUP)
            quantize(q_codes[s][:, cols], q_scales[s][:, cols], packed["q", s, g][:])

        def t1_widen(s, r):
            dst = sbuf("t1_wide%d%d" % (s, r), [P, 2 * D], BF16)
            wide[s, r], wide[s, r + 1] = dst[:, 0:D], dst[:, D : 2 * D]
            nc.vector.tensor_copy(out=dst[:], in_=bytes_sb[s][:, r : r + 2, :].rearrange("p r d -> p (r d)").bitcast(FP8))

        def t1_transpose(s, r, count):
            transpose(("t1", s, r), [wide[s, r + x] for x in range(count)])

        def t1_scale(s, r, count):
            dst = sbuf("t1_packed%d%d" % (s, r), [P, count * P * PACK], BF16)
            packed["t1", s, r] = dst
            bank = banks["t1", s, r][:, 0 : count * P * 2].bitcast(BF16)
            every_column = scale_sb[:].unsqueeze(1).to_broadcast([P, count * P, PACK])
            nc.vector.tensor_tensor(
                out=dst[:].rearrange("p (c u e) -> p c u e", u=2, e=2),
                in0=bank.rearrange("p (u c e) -> p c u e", u=2, e=2),
                in1=every_column.rearrange("p c (u e) -> p c u e", u=2),
                op=MULT,
            )

        def t1_quantize(s, r, count):
            words = sbuf("t1_codes%d%d" % (s, r), [P, count * P], U32)
            planes = sbuf("t1_scales%d%d" % (s, r), [P, count * P], U8)
            quantize(words[:], planes[:], packed["t1", s, r][:])
            for x in range(count):
                cols = slice(x * P, (x + 1) * P)
                codes["t1", s, r + x], scales["t1", s, r + x] = words[:, cols], planes[:, cols]

        def score_matmul(s, r, lo, hi):
            t = psum_bank()
            banks["score", s, r, lo] = t
            nc.tensor.matmul_mx(
                out=t[:, 0 : hi - lo],
                lhsT=codes["t1", s, r].bitcast(FP8X4),
                lhsT_scale=scales["t1", s, r],
                rhs=q_codes[s][:, lo:hi].bitcast(FP8X4),
                rhs_scale=q_scales[s][:, lo:hi],
                start=True,
                stop=True,
            )

        def score_copy(s, r, lo, hi, engine):
            src = banks["score", s, r, lo][:, 0 : hi - lo]
            dst = out_sb[s, r // 2][:, r % 2, lo:hi]
            if engine == "scalar":
                nc.scalar.activation(out=dst, in_=src, func=IDENTITY, bias=bias_sb[:])
            else:
                nc.vector.tensor_scalar(out=dst, in0=src, scalar1=bias_sb[:], scalar2=None, op0=ADD)

        out_rows = out.rearrange("b s (p r) j -> s r p b j", r=ROW_TILES)
        out_pairs = out.rearrange("b s (p x r) j -> s x p b (r j)", x=ROW_TILES // 2, r=2)

        def store(s, r, lo, hi):
            src = out_sb[s, r // 2][:, r % 2, lo:hi]
            nc.sync.dma_start(out=out_rows[s, r][:, :, lo:hi], in_=src.unsqueeze(1).to_broadcast([P, COPIES, hi - lo]))

        def store_pair(s, x):
            src = out_sb[s, x][:].rearrange("p r j -> p (r j)")
            nc.sync.dma_start(out=out_pairs[s, x], in_=src.unsqueeze(1).to_broadcast([P, COPIES, 2 * N]))

        def score_rows(s, tiles, engines, after_row):
            for x in range(len(tiles) + 1):
                if x < len(tiles):
                    for lo in (0, HALF):
                        score_matmul(s, tiles[x], lo, lo + HALF)
                if x > 0:
                    for lo, engine in zip((0, HALF), engines):
                        score_copy(s, tiles[x - 1], lo, lo + HALF, engine)
                    after_row(tiles[x - 1])

        kernel_in = kernel.rearrange("(m t) e -> m t e", t=PACK)
        tensor0_in = tensor0.rearrange("s (g p h) e -> s p g h e", p=P, h=2)
        bytes_in = tensor1_bytes.rearrange("s (p r) d -> s p r d", r=ROW_TILES)
        nc.sync.dma_start(out=bytes_sb[0][:, 0:2, :], in_=bytes_in[0][:, 0:2, :])
        for half in (0, 1):
            ts = slice(2 * half, 2 * half + 2)
            nc.sync.dma_start(out=kernel_sb[:, ts, :], in_=kernel_in[:, ts, :])
        nc.sync.dma_start(out=scale_sb[:], in_=tensor1_scale.rearrange("a b (p t) -> p (a b t)", t=PACK))
        for g in range(N // GROUP):
            nc.sync.dma_start(out=tensor0_sb[0][:, g], in_=tensor0_in[0][:, g])
        nc.sync.dma_start(out=bias_bf[:], in_=bias.partition_broadcast(P))
        nc.sync.dma_start(out=bytes_sb[0][:, 2:ROW_TILES, :], in_=bytes_in[0][:, 2:ROW_TILES, :])
        nc.sync.dma_start(out=tensor0_sb[1][:], in_=tensor0_in[1])
        nc.sync.dma_start(out=bytes_sb[1][:], in_=bytes_in[1])

        nc.vector.memset(zeros[:], 0.0)
        make_identity(nc, ident[:])
        nc.gpsimd.memset(table_in[:], 0.0)
        nc.scalar.activation(out=table_out[:], in_=table_in[:], func=IDENTITY)
        nc.gpsimd.tensor_copy(out=bias_sb[:], in_=bias_bf[:])

        spin(4)
        t1_widen(0, 0)
        kernel_transpose(0)
        spin(1)
        t1_transpose(0, 0, 1)
        t1_scale(0, 0, 1)
        kernel_copy(0, "scalar")
        kernel_transpose(1)
        spin(1)
        kernel_quantize(0)
        t0_transpose(0, 0)
        t1_transpose(0, 1, 1)
        kernel_copy(1, "scalar")
        spin(1)
        t0_transpose(0, 1)
        t1_scale(0, 1, 1)
        t0_copy(0, 0, "scalar")
        kernel_quantize(1)
        t0_transpose(0, 2)
        spin(1)
        t0_transpose(0, 3)
        t0_copy(0, 1, "scalar")
        t0_quantize(0, 0)
        t1_quantize(0, 0, 1)
        q_matmul(0, 0, 0)
        t0_quantize(0, 1)
        t1_widen(0, 2)
        t0_copy(0, 2, "scalar")
        q_matmul(0, 0, 1)
        q_matmul(0, 1, 0)
        t1_quantize(0, 1, 1)
        t0_copy(0, 3, "scalar")
        q_copy(0, 0, 0, "scalar")
        q_matmul(0, 1, 1)
        t1_transpose(0, 2, 2)
        t0_quantize(0, 2)
        t0_quantize(0, 3)
        q_matmul(0, 2, 0)
        q_copy(0, 0, 1, "scalar")
        q_copy(0, 1, 0, "scalar")
        q_copy(0, 1, 1, "scalar")
        t1_widen(0, 4)
        q_quantize(0, 0)
        t1_scale(0, 2, 2)
        q_matmul(0, 2, 1)
        q_matmul(0, 3, 0)
        q_copy(0, 2, 0, "scalar")
        q_quantize(0, 1)
        score_matmul(0, 0, 0, GROUP)
        score_matmul(0, 1, 0, GROUP)
        q_matmul(0, 3, 1)
        t1_transpose(0, 4, 2)
        score_copy(0, 0, 0, GROUP, "scalar")
        store(0, 0, 0, GROUP)
        score_copy(0, 1, 0, GROUP, "vector")
        store(0, 1, 0, GROUP)
        t1_quantize(0, 2, 2)
        score_matmul(0, 0, GROUP, HALF)
        score_matmul(0, 1, GROUP, HALF)
        q_copy(0, 2, 1, "scalar")
        q_copy(0, 3, 0, "vector")
        q_copy(0, 3, 1, "scalar")
        q_quantize(0, 2)
        score_copy(0, 0, GROUP, HALF, "scalar")
        store(0, 0, GROUP, HALF)
        q_quantize(0, 3)
        t1_scale(0, 4, 2)
        score_copy(0, 1, GROUP, HALF, "scalar")
        store(0, 1, GROUP, HALF)
        score_matmul(0, 2, 0, HALF)
        score_matmul(0, 3, 0, HALF)
        for r in (2, 3):
            score_copy(0, r, 0, HALF, "scalar")
            store(0, r, 0, HALF)
        for r in range(4):
            score_matmul(0, r, HALF, N)
        t1_widen(0, 6)
        t1_quantize(0, 4, 2)
        for r in range(4):
            score_copy(0, r, HALF, N, "vector" if r == 1 else "scalar")
            store(0, r, HALF, N)

        def store_row(r):
            store(0, r, 0, N)

        def store_second_of_pair(s):
            def after_row(r):
                if r % 2 == 1:
                    store_pair(s, r // 2)

            return after_row

        score_rows(0, [4, 5], ("scalar", "scalar"), store_row)
        for r in range(0, ROW_TILES, 2):
            t1_widen(1, r)

        units = [("t1", 0, 6)] + [("t0", 1, g) for g in range(N // GROUP)] + [("t1", 1, r) for r in range(0, ROW_TILES, 2)]
        for x in range(len(units) + 2):
            if x < len(units):
                kind, s, y = units[x]
                if kind == "t0":
                    t0_transpose(s, y)
                else:
                    t1_transpose(s, y, 2)
            if 1 <= x <= len(units):
                kind, s, y = units[x - 1]
                if kind == "t0":
                    t0_copy(s, y, "scalar")
                else:
                    t1_scale(s, y, 2)
            if x >= 2:
                kind, s, y = units[x - 2]
                if kind == "t0":
                    t0_quantize(s, y)
                else:
                    t1_quantize(s, y, 2)
            if x == len(units) - 3:
                score_rows(0, [6, 7], ("scalar", "scalar"), store_second_of_pair(0))

        for g in range(N // GROUP + 2):
            if g < N // GROUP:
                for half in (0, 1):
                    q_matmul(1, g, half)
            if 1 <= g <= N // GROUP:
                for half in (0, 1):
                    q_copy(1, g - 1, half, "scalar")
            if g >= 2:
                q_quantize(1, g - 2)

        def store_last(r):
            if r < 2:
                store(1, r, 0, N)
            elif r % 2 == 1:
                store_pair(1, r // 2)

        score_rows(1, list(range(ROW_TILES)), ("scalar", "vector"), store_last)
